import numpy as np
import ml_dtypes


def mxq(x, axis, fmt="e4m3"):
    dtype, down = {"e4m3": (ml_dtypes.float8_e4m3fn, 7), "e5m2": (ml_dtypes.float8_e5m2, 14)}[fmt]
    v = np.moveaxis(np.asarray(x, np.float32).astype(ml_dtypes.bfloat16).astype(np.float64), axis, -1)
    blocks = v.reshape(v.shape[:-1] + (-1, 32))
    amax = np.abs(blocks).max(-1, keepdims=True)
    byte = np.maximum(np.where(amax > 0, np.frexp(amax)[1] - 1 + 127, 0) - down, 1)
    scale = np.exp2(byte - 127.0)
    codes = (blocks / scale).astype(np.float32).astype(dtype).astype(np.float64)
    return np.moveaxis((codes * scale).reshape(v.shape), -1, axis)


WIDE = False


def mx_kscale(k):
    if not WIDE:
        return np.ones(k)
    levels = np.array([10, -10, 5, -5, 0])
    a = np.random.permutation(np.resize(levels, k // 512 * 4)).reshape(k // 512, 4)
    idx = np.arange(k)
    return np.exp2(a[idx // 512, idx % 128 // 32])


BF16 = ml_dtypes.bfloat16


def bf(x):
    return np.asarray(x, np.float32).astype(BF16)


def f64(x):
    return np.asarray(x).astype(np.float64)


N, F, E, H, R = 1024, 1024, 1024, 4, 8
EPS = 1e-6


def setup_inputs():
    s = mx_kscale(F)
    c = 4.0 / np.sqrt(E)
    B = np.random.standard_normal((R, E)) / np.sqrt(R)
    W = c * (0.8 * np.random.standard_normal((F, R)) @ B + 0.6 * np.random.standard_normal((F, E))) / np.sqrt(F)
    Z = c * (0.8 * np.random.standard_normal((H, N, R)) @ B + 0.6 * np.random.standard_normal((H, N, E)))
    return {"X": bf(np.random.standard_normal((N, F)) * s), "W": bf(W / s[:, None]), "Z": bf(Z),
            "beta": bf(1.5 + 0.5 * np.random.random(1))}


def reference(X, W, Z, beta):
    Zf = f64(Z)
    X_emb = mxq(f64(X), 1, "e4m3") @ mxq(f64(W), 0, "e4m3")
    aff = mxq(Zf, 2, "e4m3") @ mxq(X_emb, 1, "e4m3").T
    X_norm = np.sqrt(np.sum(X_emb * X_emb, axis=-1))
    Z_norm = np.sqrt(np.sum(Zf * Zf, axis=-1))
    aff = aff / (X_norm[None, None, :] + EPS)
    aff = aff / (Z_norm[:, :, None] + EPS)
    aff = np.max(aff, axis=0)
    aff = (aff + aff.T) / 2.0
    aff = (aff + 1.0) / 2.0
    return np.power(aff, f64(beta))

@@ -1,0 +1,496 @@
+from contextlib import ExitStack
+
+import concourse.mybir as mybir
+from concourse.masks import make_identity
+
+FLOPS = 2 * 1024 * 1024 * 1024 * 5
+
+BF16 = mybir.dt.bfloat16
+F32 = mybir.dt.float32
+U32 = mybir.dt.uint32
+U8 = mybir.dt.uint8
+FP8X4 = mybir.dt.float8_e4m3fn_x4
+ACT = mybir.ActivationFunctionType
+ALU = mybir.AluOpType
+AX = mybir.AxisListType
+P = 128
+EPS = 1e-6
+MANUAL = True
+ZBUFS = 8
+MMB = 5
+TRB = 3
+OWN = "G"
+WRE = "GSVS"
+XECP = ("VV","VV")
+XCP = ("VV","VV")
+NSQ0 = 4
+ZSQ0 = 6
+EVS = (0, 12)
+LOADS = (("x", 0), ("w", 0), ("w", 1), ("w", 2), ("w", 3), ("z", 0), ("x", 1), ("z", 1), ("z", 2), ("z", 3), ("z", 4), ("z", 5), ("z", 6), ("z", 7))
+ZSW = 12
+
+
+def span(j, hh):
+    first = 4 * hh
+    return first, min(j, first + 3) - first + 1
+
+
+def tile_affnet_t_kernel(tc, X, W, Z, beta, out):
+    nc = tc.nc
+    with ExitStack() as ctx:
+        const = ctx.enter_context(tc.tile_pool(name="const", bufs=1))
+        keep = ctx.enter_context(tc.tile_pool(name="keep", bufs=1))
+        zin = ctx.enter_context(tc.tile_pool(name="zin", bufs=ZBUFS))
+        zgp = ctx.enter_context(tc.tile_pool(name="zgp", bufs=2))
+        st = ctx.enter_context(tc.tile_pool(name="st", bufs=1))
+        xgp = ctx.enter_context(tc.tile_pool(name="xgp", bufs=3))
+        psum = ctx.enter_context(tc.psum_pool(name="psum", bufs=1))
+        taken = {"mm": 0, "tr": 0}
+
+        def bank_tile(op, kind, shape):
+            taken[kind] += 1
+            return psum.tile(shape, F32, name="bank", tag="%s%d" % (kind, taken[kind] % (MMB if kind == "mm" else TRB)))
+
+        def copy_on(which, dst, src):
+            if which == "V":
+                nc.vector.tensor_copy(out=dst, in_=src)
+            elif which == "S":
+                nc.scalar.copy(out=dst, in_=src)
+            else:
+                nc.gpsimd.tensor_scalar(out=dst, in0=src, scalar1=1.0, scalar2=0.0, op0=ALU.mult, op1=ALU.add)
+
+        ident = const.tile([P, P], F32)
+        make_identity(nc, ident[:])
+        half = const.tile([P, 8], F32)
+        nc.vector.memset(half[:], 0.5)
+        warm = const.tile([P, 1], F32)
+        nc.scalar.activation(out=warm[:], in_=half[:, 0:1], func=ACT.Ln)
+        beta_bf = const.tile([P, 1], BF16)
+        nc.scalar.dma_start(out=beta_bf[:], in_=beta.partition_broadcast(P))
+        beta_f = const.tile([P, 1], F32)
+        nc.vector.tensor_copy(out=beta_f[:], in_=beta_bf[:])
+        junk = const.tile([P, 1024], BF16)
+
+        if MANUAL:
+            ctx.enter_context(tc.manual_schedule())
+
+        zq = keep.tile([P, 8, 1024], U32, align_bytes=64)
+        zs = keep.tile([P, 8, 1024], U8, align_bytes=64)
+        xeq = keep.tile([P, 2, 1024], U32, align_bytes=64)
+        xes = keep.tile([P, 2, 1024], U8, align_bytes=64)
+        zn2 = keep.tile([P, 32], F32)
+        zn = keep.tile([P, 32], F32)
+        zne = keep.tile([P, 32], F32)
+        rz = keep.tile([P, 32], F32)
+        xn2p = keep.tile([P, 16], F32)
+        xn2 = keep.tile([P, 8], F32)
+        xn = keep.tile([P, 8], F32)
+        xne = keep.tile([P, 8], F32)
+        rx = keep.tile([P, 8], F32)
+        rxb = keep.tile([P, 1024], F32)
+        x_sb = st.tile([P, 8, 1024], BF16, name="x_sb", tag="slot_a")
+        w_raw = st.tile([P, 2, 4, 1024], BF16, name="w_raw", tag="slot_b")
+        xq = st.tile([P, 8, 256], U32, align_bytes=64)
+        xs = st.tile([P, 8, 256], U8, align_bytes=64)
+        wq = st.tile([P, 2, 1024], U32, align_bytes=64)
+        ws = st.tile([P, 2, 1024], U8, align_bytes=64)
+        xeg = st.tile([P, 2, 1024, 4], BF16, name="xeg", tag="slot_c", align_bytes=64)
+
+        t = {}
+
+        def e_zld(eng, i):
+            t[("z", i)] = zin.tile([P, 4, 1024], BF16, name="zt")
+            nc.sync.dma_start(out=t[("z", i)][:], in_=Z[:, i * P:(i + 1) * P, :].rearrange("h p k -> p h k"))
+
+        def e_xld(eng, hf):
+            nc.sync.dma_start(out=x_sb[:, 4 * hf:4 * hf + 4, :],
+                              in_=X[512 * hf:512 * (hf + 1), :].rearrange("(t p) f -> p t f", p=P))
+
+        def e_wld(eng, a):
+            nc.sync.dma_start(out=w_raw[:, a // 2, 2 * (a % 2):2 * (a % 2) + 2, :],
+                              in_=W[256 * a:256 * (a + 1), :].rearrange("(p e) c -> p e c", e=2))
+
+        def word_transposes(op, key, src_rows):
+            pt = bank_tile(op, "tr", [P, 4, P])
+            words = src_rows.bitcast(F32)
+            for a in range(4):
+                nc.tensor.transpose(pt[:, a, :], words[:, a * P:(a + 1) * P], ident[:])
+            t[key] = pt
+
+        def e_ztr(eng, i, h):
+            word_transposes(("ztr", i, h), ("zt", i, h), t[("z", i)][:, h, :])
+
+        def e_zcp(eng, i, h):
+            if ("zg", i) not in t:
+                t[("zg", i)] = zgp.tile([P, 4, 2, P, 4], BF16, name="zg", align_bytes=64)
+            copy_on(eng, t[("zg", i)][:, h].bitcast(F32), t[("zt", i, h)][:].rearrange("p (g u) n -> p g n u", u=2))
+
+        def e_zsq(eng, i, h):
+            nc.scalar.activation(out=junk[:], in_=t[("z", i)][:, h, :], func=ACT.Square,
+                                 accum_out=zn2[:, 4 * i + h:4 * i + h + 1])
+
+        def e_zq(eng, i):
+            nc.vector.quantize_mx(out=zq[:, i, :].bitcast(FP8X4), scales=zs[:, i, :],
+                                  in_=t[("zg", i)][:].rearrange("p h g n t -> p (h g n t)"))
+
+        def e_zpow(eng, i):
+            c = slice(4 * i, 4 * i + 4)
+            nc.gpsimd.tensor_tensor(out=zn[:, c], in0=zn2[:, c], in1=half[:, 0:4], op=ALU.pow)
+
+        def e_rzv(eng, i):
+            c = slice(4 * i, 4 * i + 4)
+            nc.vector.tensor_scalar_add(out=zne[:, c], in0=zn[:, c], scalar1=EPS)
+            nc.vector.reciprocal(out=rz[:, c], in_=zne[:, c])
+
+        def e_xtr(eng, mt):
+            word_transposes(("xtr", mt), ("xt", mt), x_sb[:, mt, :])
+
+        def e_xcp(eng, mt):
+            if ("xg", mt // 4) not in t:
+                t[("xg", mt // 4)] = xgp.tile([P, 4, 2, P, 4], BF16, name="xg", tag="grp", align_bytes=64)
+            copy_on(eng, t[("xg", mt // 4)][:, mt % 4].bitcast(F32),
+                    t[("xt", mt)][:].rearrange("p (g u) n -> p g n u", u=2))
+
+        def e_xq(eng, hf):
+            r = slice(4 * hf, 4 * hf + 4)
+            nc.vector.quantize_mx(out=xq[:, r, :].rearrange("p a b -> p (a b)").bitcast(FP8X4),
+                                  scales=xs[:, r, :].rearrange("p a b -> p (a b)"),
+                                  in_=t[("xg", hf)][:].rearrange("p j g n t -> p (j g n t)"))
+
+        def e_wre(eng, g, a):
+            if ("wg", g) not in t:
+                t[("wg", g)] = xgp.tile([P, 1024, 4], BF16, name="wg", tag="grp", align_bytes=64)
+            copy_on(eng, t[("wg", g)][:, 256 * a:256 * (a + 1), :].rearrange("p (f q) t -> p f q t", f=2),
+                    w_raw[:, g, :, 256 * a:256 * (a + 1)].rearrange("p t (q f) -> p f q t", f=2))
+
+        def e_wq(eng, g, c):
+            nc.vector.quantize_mx(out=wq[:, g, 512 * c:512 * (c + 1)].bitcast(FP8X4),
+                                  scales=ws[:, g, 512 * c:512 * (c + 1)],
+                                  in_=t[("wg", g)][:, 512 * c:512 * (c + 1), :].rearrange("p c t -> p (c t)"))
+
+        def e_s1t(eng, ms, big):
+            acc = bank_tile(("s1t", ms, big), "mm", [P, 4, P])
+            for tp in range(4):
+                col = (4 * big + tp) * P
+                for g in range(2):
+                    nc.tensor.matmul_mx(out=acc[:, tp, :],
+                                        lhsT=wq[:, g, col:col + P].bitcast(FP8X4),
+                                        lhsT_scale=ws[:, g, col:col + P],
+                                        rhs=xq[:, ms, g * P:(g + 1) * P].bitcast(FP8X4),
+                                        rhs_scale=xs[:, ms, g * P:(g + 1) * P],
+                                        start=(g == 0), stop=(g == 1))
+            t[("a1", ms, big)] = acc
+
+        def e_xecp(eng, ms, big):
+            copy_on(eng, xeg[:, big, ms * P:(ms + 1) * P, :], t[("a1", ms, big)][:].rearrange("p t m -> p m t"))
+
+        def e_xeq(eng, big, hh):
+            nc.vector.quantize_mx(out=xeq[:, big, 512 * hh:512 * (hh + 1)].bitcast(FP8X4),
+                                  scales=xes[:, big, 512 * hh:512 * (hh + 1)],
+                                  in_=xeg[:, big, 512 * hh:512 * (hh + 1), :].rearrange("p m t -> p (m t)"))
+
+        def e_s1n(eng, mt, eh):
+            acc = bank_tile(("s1n", mt, eh), "mm", [P, 512])
+            for g in range(2):
+                nc.tensor.matmul_mx(out=acc[:],
+                                    lhsT=xq[:, mt, g * P:(g + 1) * P].bitcast(FP8X4),
+                                    lhsT_scale=xs[:, mt, g * P:(g + 1) * P],
+                                    rhs=wq[:, g, 512 * eh:512 * (eh + 1)].bitcast(FP8X4),
+                                    rhs_scale=ws[:, g, 512 * eh:512 * (eh + 1)],
+                                    start=(g == 0), stop=(g == 1))
+            t[("an", mt, eh)] = acc
+
+        def e_xsq(eng, mt, eh):
+            nc.scalar.activation(out=junk[:, 0:512], in_=t[("an", mt, eh)][:], func=ACT.Square,
+                                 accum_out=xn2p[:, 2 * mt + eh:2 * mt + eh + 1])
+
+        def e_xn1(eng):
+            nc.vector.tensor_reduce(out=xn2[:], in_=xn2p[:].rearrange("p (m e) -> p m e", e=2), axis=AX.X,
+                                    op=ALU.add)
+
+        def e_xpow(eng):
+            nc.gpsimd.tensor_tensor(out=xn[:], in0=xn2[:], in1=half[:], op=ALU.pow)
+
+        def e_rxv(eng):
+            nc.vector.tensor_scalar_add(out=xne[:], in0=xn[:], scalar1=EPS)
+            nc.vector.reciprocal(out=rx[:], in_=xne[:])
+
+        def e_spr(eng, hh):
+            pb = bank_tile(("spr", hh), "tr", [P, 512])
+            for j in range(4):
+                mt = 4 * hh + j
+                nc.tensor.matmul(out=pb[:, j * P:(j + 1) * P], lhsT=rx[:, mt:mt + 1].to_broadcast([P, P]),
+                                 rhs=ident[:], start=True, stop=True)
+            t[("pb", hh)] = pb
+
+        def e_spc(eng, hh):
+            copy_on(eng, rxb[:, 512 * hh:512 * (hh + 1)], t[("pb", hh)][:])
+
+        def e_umm(eng, i, hh, h):
+            acc = bank_tile(("umm", i, hh, h), "mm", [P, 512])
+            for big in range(2):
+                col = (2 * h + big) * P
+                nc.tensor.matmul_mx(out=acc[:],
+                                    lhsT=zq[:, i, col:col + P].bitcast(FP8X4),
+                                    lhsT_scale=zs[:, i, col:col + P],
+                                    rhs=xeq[:, big, 512 * hh:512 * (hh + 1)].bitcast(FP8X4),
+                                    rhs_scale=xes[:, big, 512 * hh:512 * (hh + 1)],
+                                    start=(big == 0), stop=(big == 1))
+            t[("a2", i, hh, h)] = acc
+
+        def late(index):
+            if "late" not in t:
+                t["late"] = st.tile([P, 8, 512], F32, name="late", tag="slot_c", align_bytes=64)
+            return t["late"][:, index, :]
+
+        def e_ev(eng, i, hh, h):
+            acc = t[("a2", i, hh, h)]
+            sc = rz[:, 4 * i + h:4 * i + h + 1]
+            u = 2 * i + hh
+            if h == 0:
+                if eng == "V":
+                    nc.vector.tensor_scalar_mul(out=late(2 * (u % 2)), in0=acc[:], scalar1=sc)
+                else:
+                    nc.scalar.activation(out=late(2 * (u % 2)), in_=acc[:], func=ACT.Copy, scale=sc)
+                return
+            if h == 3:
+                if ("b", i) not in t:
+                    quad = st.tile([P, 4, 1024], F32, name="b_quad", tag="slot_a" if i < 4 else "slot_b")
+                    for k in range(4):
+                        t[("b", 4 * (i // 4) + k)] = quad[:, k, :]
+                dst = t[("b", i)][:, 512 * hh:512 * (hh + 1)]
+            else:
+                dst = late(2 * (u % 2) + h % 2)
+            nc.vector.scalar_tensor_tensor(out=dst, in0=acc[:], scalar=sc, in1=late(2 * (u % 2) + (h - 1) % 2),
+                                           op0=ALU.mult, op1=ALU.max)
+
+        def e_ftr(eng, j, hh):
+            first, count = span(j, hh)
+            pt = bank_tile(("ftr", j, hh), "tr", [P, 4, P])
+            for k in range(count):
+                nc.tensor.transpose(pt[:, k, :], t[("b", first + k)][:, j * P:(j + 1) * P], ident[:])
+            t[("ft", j, hh)] = pt
+
+        def own_view(j, hh):
+            order = [u for u in range(16) if span(u // 2, u % 2)[1] > 0]
+            return late(4 + order.index(2 * j + hh) % 4)
+
+        def e_own(eng, j, hh):
+            first, count = span(j, hh)
+            width = count * P
+            cols = slice(512 * hh, 512 * hh + width)
+            dst = own_view(j, hh)[:, 0:width]
+            if eng == "V":
+                nc.vector.tensor_tensor(out=dst, in0=t[("b", j)][:, cols], in1=rxb[:, cols], op=ALU.mult)
+            else:
+                nc.gpsimd.tensor_tensor(out=dst, in0=t[("b", j)][:, cols], in1=rxb[:, cols], op=ALU.mult)
+
+        def s_view(j, hh):
+            order = [u for u in range(16) if span(u // 2, u % 2)[1] > 0]
+            n = order.index(2 * j + hh)
+            if ("sq", n // 4) not in t:
+                t[("sq", n // 4)] = xgp.tile([P, 4, 512], F32, name="s4", tag="grp", align_bytes=64)
+            return t[("sq", n // 4)][:, n % 4, :]
+
+        def e_sum(eng, j, hh):
+            first, count = span(j, hh)
+            width = count * P
+            nc.vector.scalar_tensor_tensor(out=s_view(j, hh)[:, 0:width],
+                                           in0=t[("ft", j, hh)][:].rearrange("p a b -> p (a b)")[:, 0:width],
+                                           scalar=rx[:, j:j + 1], in1=own_view(j, hh)[:, 0:width],
+                                           op0=ALU.mult, op1=ALU.add)
+
+        def e_ln(eng, j, hh):
+            width = span(j, hh)[1] * P
+            s = s_view(j, hh)
+            nc.scalar.activation(out=s[:, 0:width], in_=s[:, 0:width], func=ACT.Ln, bias=0.5, scale=0.25)
+
+        def e_ex(eng, j, hh):
+            width = span(j, hh)[1] * P
+            s = s_view(j, hh)
+            nc.scalar.activation(out=s[:, 0:width], in_=s[:, 0:width], func=ACT.Exp, scale=beta_f[:, 0:1])
+
+        def e_st(eng, j, hh):
+            width = span(j, hh)[1] * P
+            nc.sync.dma_start(out=out[j * P:(j + 1) * P, 512 * hh:512 * hh + width], in_=s_view(j, hh)[:, 0:width])
+
+        def lower_of(j, hh):
+            first, count = span(j, hh)
+            return first, min(count, j - first)
+
+        def e_mtr(eng, j, hh):
+            first, lower = lower_of(j, hh)
+            po = bank_tile(("mtr", j, hh), "tr", [P, 4, P])
+            for k in range(lower):
+                nc.tensor.transpose(po[:, k, :], s_view(j, hh)[:, k * P:(k + 1) * P], ident[:])
+            t[("po", j, hh)] = po
+
+        def m_view(j, hh):
+            order = [u for u in range(16) if lower_of(u // 2, u % 2)[1] > 0]
+            n = order.index(2 * j + hh)
+            if ("mq", n // 4) not in t:
+                t[("mq", n // 4)] = zin.tile([P, 4, 512], F32, name="zt")
+            return t[("mq", n // 4)][:, n % 4, :]
+
+        def e_mcp(eng, j, hh):
+            first, lower = lower_of(j, hh)
+            copy_on(eng, m_view(j, hh)[:, 0:lower * P],
+                    t[("po", j, hh)][:].rearrange("p a b -> p (a b)")[:, 0:lower * P])
+
+        def e_mst(eng, j, hh):
+            first, lower = lower_of(j, hh)
+            nc.sync.dma_start(
+                out=out[first * P:(first + lower) * P, j * P:(j + 1) * P].rearrange("(a i) c -> i a c", i=P),
+                in_=m_view(j, hh)[:, 0:lower * P].rearrange("p (a c) -> p a c", c=P))
+
+
+        for op in LOADS:
+            if op[0] == "z":
+                e_zld("D", op[1])
+            elif op[0] == "x":
+                e_xld("D", op[1])
+            else:
+                e_wld("D", op[1])
+
+        def heads_of(z):
+            return z // 2, (2 * (z % 2), 2 * (z % 2) + 1)
+
+        def z_squares(z):
+            zi, hs = heads_of(z)
+            for h in hs:
+                e_zsq("S", zi, h)
+            if z % 2 == 1:
+                e_zpow("G", zi)
+
+        def z_turn(z):
+            zi, hs = heads_of(z)
+            for h in hs:
+                e_ztr("PE", zi, h)
+                e_zcp("S" if z >= ZSW else "V", zi, h)
+
+        def z_close(zi):
+            e_zq("V", zi)
+            e_rzv("V", zi)
+
+        def x_square(mt, eh):
+            e_s1n("PE", mt, eh)
+            e_xsq("S", mt, eh)
+
+        def fin1(u):
+            j, hh = u // 2, u % 2
+            if 0 <= u < 16 and span(j, hh)[1] > 0:
+                e_ftr("PE", j, hh)
+                e_own(OWN if u < 14 else "V", j, hh)
+                e_sum("V", j, hh)
+
+        def fin_ln(u):
+            if 0 <= u < 16 and span(u // 2, u % 2)[1] > 0:
+                e_ln("S", u // 2, u % 2)
+
+        def fin_ex(u):
+            if span(u // 2, u % 2)[1] > 0:
+                e_ex("S", u // 2, u % 2)
+                e_st("D", u // 2, u % 2)
+
+        def fin_mirror(u, who):
+            j, hh = u // 2, u % 2
+            if lower_of(j, hh)[1] > 0:
+                e_mtr("PE", j, hh)
+                e_mcp(who, j, hh)
+                e_mst("D", j, hh)
+
+        def xe_half(hf):
+            for big in range(2):
+                for ms in range(4 * hf, 4 * hf + 4):
+                    e_s1t("PE", ms, big)
+                    e_xecp(XECP[hf][ms % 2], ms, big)
+
+        def x_half(hf):
+            for m in range(4 * hf, 4 * hf + 4):
+                e_xtr("PE", m)
+                e_xcp(XCP[hf][m % 2], m)
+            e_xq("V", hf)
+
+        x_half(0)
+        for g in range(2):
+            for a in range(4):
+                e_wre(WRE[a], g, a)
+        for c in range(2):
+            for g in range(2):
+                e_wq("V", g, c)
+        z_squares(0)
+        z_squares(1)
+        xe_half(0)
+        z_turn(0)
+        x_half(1)
+        for big in range(2):
+            e_xeq("V", big, 0)
+        for mt in range(NSQ0):
+            x_square(mt, 0)
+            x_square(mt, 1)
+        z_turn(1)
+        z_squares(2)
+        z_squares(3)
+        xe_half(1)
+        z_close(0)
+        z_turn(2)
+        for big in range(2):
+            e_xeq("V", big, 1)
+        z_turn(3)
+        for z in range(4, ZSQ0):
+            z_squares(z)
+        z_close(1)
+
+        fin_from = 2 * (8 - NSQ0) + 3
+        for s in range(16):
+            i, hh = s // 2, s % 2
+            for h in range(4):
+                e_umm("PE", i, hh, h)
+            for h in range(4):
+                e_ev("S" if (h == 0 and EVS[0] <= s < EVS[1]) else "V", i, hh, h)
+            if s + 4 < 16:
+                z_turn(s + 4)
+            if s + ZSQ0 < 16:
+                z_squares(s + ZSQ0)
+            if s + 3 < 16 and (s + 3) % 2 == 1:
+                z_close((s + 3) // 2)
+            if s < 2 * (8 - NSQ0):
+                x_square(NSQ0 + s // 2, s % 2)
+            if s == fin_from - 3:
+                e_xn1("V")
+                e_xpow("G")
+            if s == fin_from - 2:
+                e_rxv("V")
+            if s == fin_from - 1:
+                for k in range(2):
+                    e_spr("PE", k)
+                    e_spc("S", k)
+            if s == fin_from:
+                for u in range(s):
+                    fin1(u)
+                for u in range(s - 1):
+                    fin_ln(u)
+            if s > fin_from:
+                fin1(s - 1)
+                if s <= 12:
+                    fin_ln(s - 2)
+            if s == 12:
+                fin_ln(11)
+                for u in range(12):
+                    fin_ex(u)
+            if s == 13:
+                for u in range(8):
+                    fin_mirror(u, "S")
+            if s == 14:
+                for u in range(8, 12):
+                    fin_mirror(u, "S")
+                fin_ln(12)
+                fin_ln(13)
+            if s == 15:
+                fin_ln(14)
+        fin1(15)
+        fin_ln(15)
+        for u in range(12, 16):
+            fin_ex(u)
+        for u in range(12, 16):
+            fin_mirror(u, "V")

@@ -17,8 +17,8 @@ P = 128
 EPS = 1e-6
 MANUAL = True
 ZBUFS = 8
-MMB = 5
-TRB = 3
+MMB = 4
+TRB = 4
 OWN = "G"
 WRE = "GSVS"
 XECP = ("VV","VV")
@@ -27,7 +27,7 @@ NSQ0 = 4
 ZSQ0 = 6
 EVS = (0, 12)
 LOADS = (("x", 0), ("w", 0), ("w", 1), ("w", 2), ("w", 3), ("z", 0), ("x", 1), ("z", 1), ("z", 2), ("z", 3), ("z", 4), ("z", 5), ("z", 6), ("z", 7))
-ZSW = 12
+ZSW = 99
 
 
 def span(j, hh):
@@ -368,6 +368,11 @@ def tile_affnet_t_kernel(tc, X, W, Z, beta, out):
                 e_ztr("PE", zi, h)
                 e_zcp("S" if z >= ZSW else "V", zi, h)
 
+        def z_ahead(z):
+            zi, hs = heads_of(z)
+            for h in hs:
+                e_ztr("PE", zi, h)
+
         def z_close(zi):
             e_zq("V", zi)
             e_rzv("V", zi)
@@ -442,18 +447,37 @@ def tile_affnet_t_kernel(tc, X, W, Z, beta, out):
         z_close(1)
 
         fin_from = 2 * (8 - NSQ0) + 3
+        z_ahead(4)
         for s in range(16):
             i, hh = s // 2, s % 2
             for h in range(4):
                 e_umm("PE", i, hh, h)
+            if s + 5 < 16:
+                z_ahead(s + 5)
+            between = []
+            if s + 4 < 16:
+                zi, hs = heads_of(s + 4)
+                for h in hs:
+                    if s + 4 >= ZSW:
+                        e_zcp("S", zi, h)
+                    else:
+                        between.append(("zcp", zi, h))
+            if s > fin_from:
+                between.append(("fin", s - 1, 0))
+            if s + 3 < 16 and (s + 3) % 2 == 1:
+                between.append(("close", (s + 3) // 2, 0))
             for h in range(4):
                 e_ev("S" if (h == 0 and EVS[0] <= s < EVS[1]) else "V", i, hh, h)
-            if s + 4 < 16:
-                z_turn(s + 4)
+                if h >= 1 and h - 1 < len(between):
+                    job = between[h - 1]
+                    if job[0] == "zcp":
+                        e_zcp("V", job[1], job[2])
+                    elif job[0] == "fin":
+                        fin1(job[1])
+                    else:
+                        z_close(job[1])
             if s + ZSQ0 < 16:
                 z_squares(s + ZSQ0)
-            if s + 3 < 16 and (s + 3) % 2 == 1:
-                z_close((s + 3) // 2)
             if s < 2 * (8 - NSQ0):
                 x_square(NSQ0 + s // 2, s % 2)
             if s == fin_from - 3:
@@ -470,10 +494,8 @@ def tile_affnet_t_kernel(tc, X, W, Z, beta, out):
                     fin1(u)
                 for u in range(s - 1):
                     fin_ln(u)
-            if s > fin_from:
-                fin1(s - 1)
-                if s <= 12:
-                    fin_ln(s - 2)
+            if s > fin_from and s <= 12:
+                fin_ln(s - 2)
             if s == 12:
                 fin_ln(11)
                 for u in range(12):

@@ -28,6 +28,8 @@ ZSQ0 = 6
 EVS = (0, 12)
 LOADS = (("x", 0), ("w", 0), ("w", 1), ("w", 2), ("w", 3), ("z", 0), ("x", 1), ("z", 1), ("z", 2), ("z", 3), ("z", 4), ("z", 5), ("z", 6), ("z", 7))
 ZSW = 99
+ZS1 = (0, 0)
+PEO = "0123ab"
 
 
 def span(j, hh):
@@ -63,12 +65,13 @@ def tile_affnet_t_kernel(tc, X, W, Z, beta, out):
         make_identity(nc, ident[:])
         half = const.tile([P, 8], F32)
         nc.vector.memset(half[:], 0.5)
+        minus = const.tile([P, 8], F32)
+        nc.vector.memset(minus[:], -1.0)
         warm = const.tile([P, 1], F32)
         nc.scalar.activation(out=warm[:], in_=half[:, 0:1], func=ACT.Ln)
         beta_bf = const.tile([P, 1], BF16)
         nc.scalar.dma_start(out=beta_bf[:], in_=beta.partition_broadcast(P))
         beta_f = const.tile([P, 1], F32)
-        nc.vector.tensor_copy(out=beta_f[:], in_=beta_bf[:])
         junk = const.tile([P, 1024], BF16)
 
         if MANUAL:
@@ -103,6 +106,10 @@ def tile_affnet_t_kernel(tc, X, W, Z, beta, out):
             nc.sync.dma_start(out=t[("z", i)][:], in_=Z[:, i * P:(i + 1) * P, :].rearrange("h p k -> p h k"))
 
         def e_xld(eng, hf):
+            if hf == 0:
+                for m in range(4):
+                    nc.sync.dma_start(out=x_sb[:, m, :], in_=X[m * P:(m + 1) * P, :])
+                return
             nc.sync.dma_start(out=x_sb[:, 4 * hf:4 * hf + 4, :],
                               in_=X[512 * hf:512 * (hf + 1), :].rearrange("(t p) f -> p t f", p=P))
 
@@ -136,11 +143,11 @@ def tile_affnet_t_kernel(tc, X, W, Z, beta, out):
         def e_zpow(eng, i):
             c = slice(4 * i, 4 * i + 4)
             nc.gpsimd.tensor_tensor(out=zn[:, c], in0=zn2[:, c], in1=half[:, 0:4], op=ALU.pow)
+            nc.gpsimd.tensor_scalar(out=zne[:, c], in0=zn[:, c], scalar1=EPS, scalar2=1.0, op0=ALU.add, op1=ALU.mult)
+            nc.gpsimd.tensor_tensor(out=rz[:, c], in0=zne[:, c], in1=minus[:, 0:4], op=ALU.pow)
 
         def e_rzv(eng, i):
-            c = slice(4 * i, 4 * i + 4)
-            nc.vector.tensor_scalar_add(out=zne[:, c], in0=zn[:, c], scalar1=EPS)
-            nc.vector.reciprocal(out=rz[:, c], in_=zne[:, c])
+            return
 
         def e_xtr(eng, mt):
             word_transposes(("xtr", mt), ("xt", mt), x_sb[:, mt, :])
@@ -205,15 +212,16 @@ def tile_affnet_t_kernel(tc, X, W, Z, beta, out):
                                  accum_out=xn2p[:, 2 * mt + eh:2 * mt + eh + 1])
 
         def e_xn1(eng):
-            nc.vector.tensor_reduce(out=xn2[:], in_=xn2p[:].rearrange("p (m e) -> p m e", e=2), axis=AX.X,
-                                    op=ALU.add)
+            pairs = xn2p[:].rearrange("p (m e) -> p m e", e=2)
+            nc.gpsimd.tensor_tensor(out=xn2[:], in0=pairs[:, :, 0], in1=pairs[:, :, 1], op=ALU.add)
 
         def e_xpow(eng):
             nc.gpsimd.tensor_tensor(out=xn[:], in0=xn2[:], in1=half[:], op=ALU.pow)
+            nc.gpsimd.tensor_scalar(out=xne[:], in0=xn[:], scalar1=EPS, scalar2=1.0, op0=ALU.add, op1=ALU.mult)
+            nc.gpsimd.tensor_tensor(out=rx[:], in0=xne[:], in1=minus[:], op=ALU.pow)
 
         def e_rxv(eng):
-            nc.vector.tensor_scalar_add(out=xne[:], in0=xn[:], scalar1=EPS)
-            nc.vector.reciprocal(out=rx[:], in_=xne[:])
+            return
 
         def e_spr(eng, hh):
             pb = bank_tile(("spr", hh), "tr", [P, 512])
@@ -444,21 +452,22 @@ def tile_affnet_t_kernel(tc, X, W, Z, beta, out):
         z_turn(3)
         for z in range(4, ZSQ0):
             z_squares(z)
-        z_close(1)
 
         fin_from = 2 * (8 - NSQ0) + 3
         z_ahead(4)
         for s in range(16):
             i, hh = s // 2, s % 2
-            for h in range(4):
-                e_umm("PE", i, hh, h)
-            if s + 5 < 16:
-                z_ahead(s + 5)
+            for c in PEO:
+                if c in "0123":
+                    e_umm("PE", i, hh, int(c))
+                elif s + 5 < 16:
+                    zi, hs = heads_of(s + 5)
+                    e_ztr("PE", zi, hs[0 if c == "a" else 1])
             between = []
             if s + 4 < 16:
                 zi, hs = heads_of(s + 4)
                 for h in hs:
-                    if s + 4 >= ZSW:
+                    if s + 4 >= ZSW or (h % 2 == 1 and ZS1[0] <= s < ZS1[1]):
                         e_zcp("S", zi, h)
                     else:
                         between.append(("zcp", zi, h))
@@ -480,6 +489,8 @@ def tile_affnet_t_kernel(tc, X, W, Z, beta, out):
                 z_squares(s + ZSQ0)
             if s < 2 * (8 - NSQ0):
                 x_square(NSQ0 + s // 2, s % 2)
+            if s == 8:
+                nc.gpsimd.tensor_copy(out=beta_f[:], in_=beta_bf[:])
             if s == fin_from - 3:
                 e_xn1("V")
                 e_xpow("G")
@@ -498,9 +509,11 @@ def tile_affnet_t_kernel(tc, X, W, Z, beta, out):
                 fin_ln(s - 2)
             if s == 12:
                 fin_ln(11)
-                for u in range(12):
+                for u in range(8):
                     fin_ex(u)
             if s == 13:
+                for u in range(8, 12):
+                    fin_ex(u)
                 for u in range(8):
                     fin_mirror(u, "S")
             if s == 14:

@@ -16,7 +16,7 @@ AX = mybir.AxisListType
 P = 128
 EPS = 1e-6
 MANUAL = True
-ZBUFS = 8
+ZBUFS = 7
 MMB = 4
 TRB = 4
 OWN = "G"
@@ -26,7 +26,7 @@ XCP = ("VV","VV")
 NSQ0 = 4
 ZSQ0 = 6
 EVS = (0, 12)
-LOADS = (("x", 0), ("w", 0), ("w", 1), ("w", 2), ("w", 3), ("z", 0), ("x", 1), ("z", 1), ("z", 2), ("z", 3), ("z", 4), ("z", 5), ("z", 6), ("z", 7))
+LOADS = (("x", 0), ("w", 0), ("w", 1), ("w", 2), ("w", 3), ("z", 0), ("x", 1), ("z", 1), ("z", 2), ("z", 3), ("z", 4), ("z", 5), ("z", 6))
 ZSW = 99
 ZS1 = (0, 0)
 PEO = "0123ab"
@@ -72,7 +72,12 @@ def tile_affnet_t_kernel(tc, X, W, Z, beta, out):
         beta_bf = const.tile([P, 1], BF16)
         nc.scalar.dma_start(out=beta_bf[:], in_=beta.partition_broadcast(P))
         beta_f = const.tile([P, 1], F32)
-        junk = const.tile([P, 1024], BF16)
+        junks = const.tile([P, 4, 1024], BF16)
+        spent = [0]
+
+        def junk():
+            spent[0] += 1
+            return junks[:, spent[0] % 4, :]
 
         if MANUAL:
             ctx.enter_context(tc.manual_schedule())
@@ -133,7 +138,7 @@ def tile_affnet_t_kernel(tc, X, W, Z, beta, out):
             copy_on(eng, t[("zg", i)][:, h].bitcast(F32), t[("zt", i, h)][:].rearrange("p (g u) n -> p g n u", u=2))
 
         def e_zsq(eng, i, h):
-            nc.scalar.activation(out=junk[:], in_=t[("z", i)][:, h, :], func=ACT.Square,
+            nc.scalar.activation(out=junk(), in_=t[("z", i)][:, h, :], func=ACT.Square,
                                  accum_out=zn2[:, 4 * i + h:4 * i + h + 1])
 
         def e_zq(eng, i):
@@ -208,7 +213,7 @@ def tile_affnet_t_kernel(tc, X, W, Z, beta, out):
             t[("an", mt, eh)] = acc
 
         def e_xsq(eng, mt, eh):
-            nc.scalar.activation(out=junk[:, 0:512], in_=t[("an", mt, eh)][:], func=ACT.Square,
+            nc.scalar.activation(out=junk()[:, 0:512], in_=t[("an", mt, eh)][:], func=ACT.Square,
                                  accum_out=xn2p[:, 2 * mt + eh:2 * mt + eh + 1])
 
         def e_xn1(eng):
@@ -442,6 +447,7 @@ def tile_affnet_t_kernel(tc, X, W, Z, beta, out):
             x_square(mt, 0)
             x_square(mt, 1)
         z_turn(1)
+        e_zld("D", 7)
         z_squares(2)
         z_squares(3)
         xe_half(1)

@@ -12,29 +12,17 @@ U8 = mybir.dt.uint8
 FP8X4 = mybir.dt.float8_e4m3fn_x4
 ACT = mybir.ActivationFunctionType
 ALU = mybir.AluOpType
-AX = mybir.AxisListType
 P = 128
 EPS = 1e-6
-MANUAL = True
-ZBUFS = 7
-MMB = 4
-TRB = 4
-OWN = "G"
-WRE = "GSVS"
-XECP = ("VV","VV")
-XCP = ("VV","VV")
-NSQ0 = 4
-ZSQ0 = 6
-EVS = (0, 12)
-LOADS = (("x", 0), ("w", 0), ("w", 1), ("w", 2), ("w", 3), ("z", 0), ("x", 1), ("z", 1), ("z", 2), ("z", 3), ("z", 4), ("z", 5), ("z", 6))
-ZSW = 99
-ZS1 = (0, 0)
-PEO = "0123ab"
+BANKS = 4
+Z_BUFFERS = 7
+SUMS_FROM = 11
+FIRST_BATCH = 12
 
 
-def span(j, hh):
-    first = 4 * hh
-    return first, min(j, first + 3) - first + 1
+def blocks_of(s):
+    first = 4 * (s % 2)
+    return first, max(0, min(s // 2, first + 3) - first + 1)
 
 
 def tile_affnet_t_kernel(tc, X, W, Z, beta, out):
@@ -42,21 +30,22 @@ def tile_affnet_t_kernel(tc, X, W, Z, beta, out):
     with ExitStack() as ctx:
         const = ctx.enter_context(tc.tile_pool(name="const", bufs=1))
         keep = ctx.enter_context(tc.tile_pool(name="keep", bufs=1))
-        zin = ctx.enter_context(tc.tile_pool(name="zin", bufs=ZBUFS))
-        zgp = ctx.enter_context(tc.tile_pool(name="zgp", bufs=2))
-        st = ctx.enter_context(tc.tile_pool(name="st", bufs=1))
-        xgp = ctx.enter_context(tc.tile_pool(name="xgp", bufs=3))
+        z_pool = ctx.enter_context(tc.tile_pool(name="z_pool", bufs=Z_BUFFERS))
+        zg_pool = ctx.enter_context(tc.tile_pool(name="zg_pool", bufs=2))
+        shared = ctx.enter_context(tc.tile_pool(name="shared", bufs=1))
+        group_pool = ctx.enter_context(tc.tile_pool(name="group_pool", bufs=3))
         psum = ctx.enter_context(tc.psum_pool(name="psum", bufs=1))
-        taken = {"mm": 0, "tr": 0}
 
-        def bank_tile(op, kind, shape):
+        taken = {"mx": 0, "tr": 0}
+
+        def bank(kind, shape):
             taken[kind] += 1
-            return psum.tile(shape, F32, name="bank", tag="%s%d" % (kind, taken[kind] % (MMB if kind == "mm" else TRB)))
+            return psum.tile(shape, F32, name="bank", tag="%s%d" % (kind, taken[kind] % BANKS))
 
-        def copy_on(which, dst, src):
-            if which == "V":
+        def copy(engine, dst, src):
+            if engine == "vector":
                 nc.vector.tensor_copy(out=dst, in_=src)
-            elif which == "S":
+            elif engine == "scalar":
                 nc.scalar.copy(out=dst, in_=src)
             else:
                 nc.gpsimd.tensor_scalar(out=dst, in0=src, scalar1=1.0, scalar2=0.0, op0=ALU.mult, op1=ALU.add)
@@ -65,473 +54,373 @@ def tile_affnet_t_kernel(tc, X, W, Z, beta, out):
         make_identity(nc, ident[:])
         half = const.tile([P, 8], F32)
         nc.vector.memset(half[:], 0.5)
-        minus = const.tile([P, 8], F32)
-        nc.vector.memset(minus[:], -1.0)
+        minus_one = const.tile([P, 8], F32)
+        nc.vector.memset(minus_one[:], -1.0)
         warm = const.tile([P, 1], F32)
         nc.scalar.activation(out=warm[:], in_=half[:, 0:1], func=ACT.Ln)
         beta_bf = const.tile([P, 1], BF16)
         nc.scalar.dma_start(out=beta_bf[:], in_=beta.partition_broadcast(P))
         beta_f = const.tile([P, 1], F32)
-        junks = const.tile([P, 4, 1024], BF16)
-        spent = [0]
+        unwanted = const.tile([P, 4, 1024], BF16)
+        squares_made = [0]
 
-        def junk():
-            spent[0] += 1
-            return junks[:, spent[0] % 4, :]
+        def scratch():
+            squares_made[0] += 1
+            return unwanted[:, squares_made[0] % 4, :]
 
-        if MANUAL:
-            ctx.enter_context(tc.manual_schedule())
+        ctx.enter_context(tc.manual_schedule())
 
-        zq = keep.tile([P, 8, 1024], U32, align_bytes=64)
-        zs = keep.tile([P, 8, 1024], U8, align_bytes=64)
-        xeq = keep.tile([P, 2, 1024], U32, align_bytes=64)
-        xes = keep.tile([P, 2, 1024], U8, align_bytes=64)
-        zn2 = keep.tile([P, 32], F32)
-        zn = keep.tile([P, 32], F32)
-        zne = keep.tile([P, 32], F32)
+        z_words = keep.tile([P, 8, 1024], U32, align_bytes=64)
+        z_scales = keep.tile([P, 8, 1024], U8, align_bytes=64)
+        xe_words = keep.tile([P, 2, 1024], U32, align_bytes=64)
+        xe_scales = keep.tile([P, 2, 1024], U8, align_bytes=64)
+        z_sq = keep.tile([P, 32], F32)
+        z_norm = keep.tile([P, 32], F32)
+        z_norm_eps = keep.tile([P, 32], F32)
         rz = keep.tile([P, 32], F32)
-        xn2p = keep.tile([P, 16], F32)
-        xn2 = keep.tile([P, 8], F32)
-        xn = keep.tile([P, 8], F32)
-        xne = keep.tile([P, 8], F32)
+        x_sq_halves = keep.tile([P, 16], F32)
+        x_sq = keep.tile([P, 8], F32)
+        x_norm = keep.tile([P, 8], F32)
+        x_norm_eps = keep.tile([P, 8], F32)
         rx = keep.tile([P, 8], F32)
-        rxb = keep.tile([P, 1024], F32)
-        x_sb = st.tile([P, 8, 1024], BF16, name="x_sb", tag="slot_a")
-        w_raw = st.tile([P, 2, 4, 1024], BF16, name="w_raw", tag="slot_b")
-        xq = st.tile([P, 8, 256], U32, align_bytes=64)
-        xs = st.tile([P, 8, 256], U8, align_bytes=64)
-        wq = st.tile([P, 2, 1024], U32, align_bytes=64)
-        ws = st.tile([P, 2, 1024], U8, align_bytes=64)
-        xeg = st.tile([P, 2, 1024, 4], BF16, name="xeg", tag="slot_c", align_bytes=64)
+        rx_row = keep.tile([P, 1024], F32)
+        x_rows = shared.tile([P, 8, 1024], BF16, name="x_rows", tag="slot_a")
+        w_rows = shared.tile([P, 2, 4, 1024], BF16, name="w_rows", tag="slot_b")
+        x_words = shared.tile([P, 8, 256], U32, align_bytes=64)
+        x_scales = shared.tile([P, 8, 256], U8, align_bytes=64)
+        w_words = shared.tile([P, 2, 1024], U32, align_bytes=64)
+        w_scales = shared.tile([P, 2, 1024], U8, align_bytes=64)
+        xe_groups = shared.tile([P, 2, 1024, 4], BF16, name="xe_groups", tag="slot_c", align_bytes=64)
 
-        t = {}
+        z_rows = {}
+        z_groups = {}
+        x_groups = {}
+        w_groups = {}
+        banks = {}
+        b = {}
+        late = {}
 
-        def e_zld(eng, i):
-            t[("z", i)] = zin.tile([P, 4, 1024], BF16, name="zt")
-            nc.sync.dma_start(out=t[("z", i)][:], in_=Z[:, i * P:(i + 1) * P, :].rearrange("h p k -> p h k"))
+        def load_x_tile(m):
+            nc.sync.dma_start(out=x_rows[:, m, :], in_=X[m * P:(m + 1) * P, :])
 
-        def e_xld(eng, hf):
-            if hf == 0:
-                for m in range(4):
-                    nc.sync.dma_start(out=x_sb[:, m, :], in_=X[m * P:(m + 1) * P, :])
-                return
-            nc.sync.dma_start(out=x_sb[:, 4 * hf:4 * hf + 4, :],
-                              in_=X[512 * hf:512 * (hf + 1), :].rearrange("(t p) f -> p t f", p=P))
+        def load_x_second_half():
+            nc.sync.dma_start(out=x_rows[:, 4:8, :], in_=X[512:1024, :].rearrange("(t p) f -> p t f", p=P))
 
-        def e_wld(eng, a):
-            nc.sync.dma_start(out=w_raw[:, a // 2, 2 * (a % 2):2 * (a % 2) + 2, :],
+        def load_w_quarter(a):
+            nc.sync.dma_start(out=w_rows[:, a // 2, 2 * (a % 2):2 * (a % 2) + 2, :],
                               in_=W[256 * a:256 * (a + 1), :].rearrange("(p e) c -> p e c", e=2))
 
-        def word_transposes(op, key, src_rows):
-            pt = bank_tile(op, "tr", [P, 4, P])
-            words = src_rows.bitcast(F32)
+        def load_z(i):
+            z_rows[i] = z_pool.tile([P, 4, 1024], BF16, name="z_tile")
+            nc.sync.dma_start(out=z_rows[i][:], in_=Z[:, i * P:(i + 1) * P, :].rearrange("h p k -> p h k"))
+
+        def transpose_words(key, rows):
+            words = rows.bitcast(F32)
+            banks[key] = bank("tr", [P, 4, P])
             for a in range(4):
-                nc.tensor.transpose(pt[:, a, :], words[:, a * P:(a + 1) * P], ident[:])
-            t[key] = pt
+                nc.tensor.transpose(banks[key][:, a, :], words[:, a * P:(a + 1) * P], ident[:])
 
-        def e_ztr(eng, i, h):
-            word_transposes(("ztr", i, h), ("zt", i, h), t[("z", i)][:, h, :])
+        def words_side_by_side(engine, dst, key):
+            copy(engine, dst.bitcast(F32), banks[key][:].rearrange("p (g u) n -> p g n u", u=2))
 
-        def e_zcp(eng, i, h):
-            if ("zg", i) not in t:
-                t[("zg", i)] = zgp.tile([P, 4, 2, P, 4], BF16, name="zg", align_bytes=64)
-            copy_on(eng, t[("zg", i)][:, h].bitcast(F32), t[("zt", i, h)][:].rearrange("p (g u) n -> p g n u", u=2))
-
-        def e_zsq(eng, i, h):
-            nc.scalar.activation(out=junk(), in_=t[("z", i)][:, h, :], func=ACT.Square,
-                                 accum_out=zn2[:, 4 * i + h:4 * i + h + 1])
-
-        def e_zq(eng, i):
-            nc.vector.quantize_mx(out=zq[:, i, :].bitcast(FP8X4), scales=zs[:, i, :],
-                                  in_=t[("zg", i)][:].rearrange("p h g n t -> p (h g n t)"))
-
-        def e_zpow(eng, i):
-            c = slice(4 * i, 4 * i + 4)
-            nc.gpsimd.tensor_tensor(out=zn[:, c], in0=zn2[:, c], in1=half[:, 0:4], op=ALU.pow)
-            nc.gpsimd.tensor_scalar(out=zne[:, c], in0=zn[:, c], scalar1=EPS, scalar2=1.0, op0=ALU.add, op1=ALU.mult)
-            nc.gpsimd.tensor_tensor(out=rz[:, c], in0=zne[:, c], in1=minus[:, 0:4], op=ALU.pow)
-
-        def e_rzv(eng, i):
-            return
-
-        def e_xtr(eng, mt):
-            word_transposes(("xtr", mt), ("xt", mt), x_sb[:, mt, :])
-
-        def e_xcp(eng, mt):
-            if ("xg", mt // 4) not in t:
-                t[("xg", mt // 4)] = xgp.tile([P, 4, 2, P, 4], BF16, name="xg", tag="grp", align_bytes=64)
-            copy_on(eng, t[("xg", mt // 4)][:, mt % 4].bitcast(F32),
-                    t[("xt", mt)][:].rearrange("p (g u) n -> p g n u", u=2))
-
-        def e_xq(eng, hf):
-            r = slice(4 * hf, 4 * hf + 4)
-            nc.vector.quantize_mx(out=xq[:, r, :].rearrange("p a b -> p (a b)").bitcast(FP8X4),
-                                  scales=xs[:, r, :].rearrange("p a b -> p (a b)"),
-                                  in_=t[("xg", hf)][:].rearrange("p j g n t -> p (j g n t)"))
-
-        def e_wre(eng, g, a):
-            if ("wg", g) not in t:
-                t[("wg", g)] = xgp.tile([P, 1024, 4], BF16, name="wg", tag="grp", align_bytes=64)
-            copy_on(eng, t[("wg", g)][:, 256 * a:256 * (a + 1), :].rearrange("p (f q) t -> p f q t", f=2),
-                    w_raw[:, g, :, 256 * a:256 * (a + 1)].rearrange("p t (q f) -> p f q t", f=2))
-
-        def e_wq(eng, g, c):
-            nc.vector.quantize_mx(out=wq[:, g, 512 * c:512 * (c + 1)].bitcast(FP8X4),
-                                  scales=ws[:, g, 512 * c:512 * (c + 1)],
-                                  in_=t[("wg", g)][:, 512 * c:512 * (c + 1), :].rearrange("p c t -> p (c t)"))
-
-        def e_s1t(eng, ms, big):
-            acc = bank_tile(("s1t", ms, big), "mm", [P, 4, P])
-            for tp in range(4):
-                col = (4 * big + tp) * P
-                for g in range(2):
-                    nc.tensor.matmul_mx(out=acc[:, tp, :],
-                                        lhsT=wq[:, g, col:col + P].bitcast(FP8X4),
-                                        lhsT_scale=ws[:, g, col:col + P],
-                                        rhs=xq[:, ms, g * P:(g + 1) * P].bitcast(FP8X4),
-                                        rhs_scale=xs[:, ms, g * P:(g + 1) * P],
-                                        start=(g == 0), stop=(g == 1))
-            t[("a1", ms, big)] = acc
-
-        def e_xecp(eng, ms, big):
-            copy_on(eng, xeg[:, big, ms * P:(ms + 1) * P, :], t[("a1", ms, big)][:].rearrange("p t m -> p m t"))
-
-        def e_xeq(eng, big, hh):
-            nc.vector.quantize_mx(out=xeq[:, big, 512 * hh:512 * (hh + 1)].bitcast(FP8X4),
-                                  scales=xes[:, big, 512 * hh:512 * (hh + 1)],
-                                  in_=xeg[:, big, 512 * hh:512 * (hh + 1), :].rearrange("p m t -> p (m t)"))
-
-        def e_s1n(eng, mt, eh):
-            acc = bank_tile(("s1n", mt, eh), "mm", [P, 512])
-            for g in range(2):
-                nc.tensor.matmul_mx(out=acc[:],
-                                    lhsT=xq[:, mt, g * P:(g + 1) * P].bitcast(FP8X4),
-                                    lhsT_scale=xs[:, mt, g * P:(g + 1) * P],
-                                    rhs=wq[:, g, 512 * eh:512 * (eh + 1)].bitcast(FP8X4),
-                                    rhs_scale=ws[:, g, 512 * eh:512 * (eh + 1)],
-                                    start=(g == 0), stop=(g == 1))
-            t[("an", mt, eh)] = acc
-
-        def e_xsq(eng, mt, eh):
-            nc.scalar.activation(out=junk()[:, 0:512], in_=t[("an", mt, eh)][:], func=ACT.Square,
-                                 accum_out=xn2p[:, 2 * mt + eh:2 * mt + eh + 1])
-
-        def e_xn1(eng):
-            pairs = xn2p[:].rearrange("p (m e) -> p m e", e=2)
-            nc.gpsimd.tensor_tensor(out=xn2[:], in0=pairs[:, :, 0], in1=pairs[:, :, 1], op=ALU.add)
-
-        def e_xpow(eng):
-            nc.gpsimd.tensor_tensor(out=xn[:], in0=xn2[:], in1=half[:], op=ALU.pow)
-            nc.gpsimd.tensor_scalar(out=xne[:], in0=xn[:], scalar1=EPS, scalar2=1.0, op0=ALU.add, op1=ALU.mult)
-            nc.gpsimd.tensor_tensor(out=rx[:], in0=xne[:], in1=minus[:], op=ALU.pow)
-
-        def e_rxv(eng):
-            return
-
-        def e_spr(eng, hh):
-            pb = bank_tile(("spr", hh), "tr", [P, 512])
-            for j in range(4):
-                mt = 4 * hh + j
-                nc.tensor.matmul(out=pb[:, j * P:(j + 1) * P], lhsT=rx[:, mt:mt + 1].to_broadcast([P, P]),
-                                 rhs=ident[:], start=True, stop=True)
-            t[("pb", hh)] = pb
-
-        def e_spc(eng, hh):
-            copy_on(eng, rxb[:, 512 * hh:512 * (hh + 1)], t[("pb", hh)][:])
-
-        def e_umm(eng, i, hh, h):
-            acc = bank_tile(("umm", i, hh, h), "mm", [P, 512])
-            for big in range(2):
-                col = (2 * h + big) * P
-                nc.tensor.matmul_mx(out=acc[:],
-                                    lhsT=zq[:, i, col:col + P].bitcast(FP8X4),
-                                    lhsT_scale=zs[:, i, col:col + P],
-                                    rhs=xeq[:, big, 512 * hh:512 * (hh + 1)].bitcast(FP8X4),
-                                    rhs_scale=xes[:, big, 512 * hh:512 * (hh + 1)],
-                                    start=(big == 0), stop=(big == 1))
-            t[("a2", i, hh, h)] = acc
-
-        def late(index):
-            if "late" not in t:
-                t["late"] = st.tile([P, 8, 512], F32, name="late", tag="slot_c", align_bytes=64)
-            return t["late"][:, index, :]
-
-        def e_ev(eng, i, hh, h):
-            acc = t[("a2", i, hh, h)]
-            sc = rz[:, 4 * i + h:4 * i + h + 1]
-            u = 2 * i + hh
-            if h == 0:
-                if eng == "V":
-                    nc.vector.tensor_scalar_mul(out=late(2 * (u % 2)), in0=acc[:], scalar1=sc)
-                else:
-                    nc.scalar.activation(out=late(2 * (u % 2)), in_=acc[:], func=ACT.Copy, scale=sc)
-                return
-            if h == 3:
-                if ("b", i) not in t:
-                    quad = st.tile([P, 4, 1024], F32, name="b_quad", tag="slot_a" if i < 4 else "slot_b")
-                    for k in range(4):
-                        t[("b", 4 * (i // 4) + k)] = quad[:, k, :]
-                dst = t[("b", i)][:, 512 * hh:512 * (hh + 1)]
-            else:
-                dst = late(2 * (u % 2) + h % 2)
-            nc.vector.scalar_tensor_tensor(out=dst, in0=acc[:], scalar=sc, in1=late(2 * (u % 2) + (h - 1) % 2),
-                                           op0=ALU.mult, op1=ALU.max)
-
-        def e_ftr(eng, j, hh):
-            first, count = span(j, hh)
-            pt = bank_tile(("ftr", j, hh), "tr", [P, 4, P])
-            for k in range(count):
-                nc.tensor.transpose(pt[:, k, :], t[("b", first + k)][:, j * P:(j + 1) * P], ident[:])
-            t[("ft", j, hh)] = pt
-
-        def own_view(j, hh):
-            order = [u for u in range(16) if span(u // 2, u % 2)[1] > 0]
-            return late(4 + order.index(2 * j + hh) % 4)
-
-        def e_own(eng, j, hh):
-            first, count = span(j, hh)
-            width = count * P
-            cols = slice(512 * hh, 512 * hh + width)
-            dst = own_view(j, hh)[:, 0:width]
-            if eng == "V":
-                nc.vector.tensor_tensor(out=dst, in0=t[("b", j)][:, cols], in1=rxb[:, cols], op=ALU.mult)
-            else:
-                nc.gpsimd.tensor_tensor(out=dst, in0=t[("b", j)][:, cols], in1=rxb[:, cols], op=ALU.mult)
-
-        def s_view(j, hh):
-            order = [u for u in range(16) if span(u // 2, u % 2)[1] > 0]
-            n = order.index(2 * j + hh)
-            if ("sq", n // 4) not in t:
-                t[("sq", n // 4)] = xgp.tile([P, 4, 512], F32, name="s4", tag="grp", align_bytes=64)
-            return t[("sq", n // 4)][:, n % 4, :]
-
-        def e_sum(eng, j, hh):
-            first, count = span(j, hh)
-            width = count * P
-            nc.vector.scalar_tensor_tensor(out=s_view(j, hh)[:, 0:width],
-                                           in0=t[("ft", j, hh)][:].rearrange("p a b -> p (a b)")[:, 0:width],
-                                           scalar=rx[:, j:j + 1], in1=own_view(j, hh)[:, 0:width],
-                                           op0=ALU.mult, op1=ALU.add)
-
-        def e_ln(eng, j, hh):
-            width = span(j, hh)[1] * P
-            s = s_view(j, hh)
-            nc.scalar.activation(out=s[:, 0:width], in_=s[:, 0:width], func=ACT.Ln, bias=0.5, scale=0.25)
-
-        def e_ex(eng, j, hh):
-            width = span(j, hh)[1] * P
-            s = s_view(j, hh)
-            nc.scalar.activation(out=s[:, 0:width], in_=s[:, 0:width], func=ACT.Exp, scale=beta_f[:, 0:1])
-
-        def e_st(eng, j, hh):
-            width = span(j, hh)[1] * P
-            nc.sync.dma_start(out=out[j * P:(j + 1) * P, 512 * hh:512 * hh + width], in_=s_view(j, hh)[:, 0:width])
-
-        def lower_of(j, hh):
-            first, count = span(j, hh)
-            return first, min(count, j - first)
-
-        def e_mtr(eng, j, hh):
-            first, lower = lower_of(j, hh)
-            po = bank_tile(("mtr", j, hh), "tr", [P, 4, P])
-            for k in range(lower):
-                nc.tensor.transpose(po[:, k, :], s_view(j, hh)[:, k * P:(k + 1) * P], ident[:])
-            t[("po", j, hh)] = po
-
-        def m_view(j, hh):
-            order = [u for u in range(16) if lower_of(u // 2, u % 2)[1] > 0]
-            n = order.index(2 * j + hh)
-            if ("mq", n // 4) not in t:
-                t[("mq", n // 4)] = zin.tile([P, 4, 512], F32, name="zt")
-            return t[("mq", n // 4)][:, n % 4, :]
-
-        def e_mcp(eng, j, hh):
-            first, lower = lower_of(j, hh)
-            copy_on(eng, m_view(j, hh)[:, 0:lower * P],
-                    t[("po", j, hh)][:].rearrange("p a b -> p (a b)")[:, 0:lower * P])
-
-        def e_mst(eng, j, hh):
-            first, lower = lower_of(j, hh)
-            nc.sync.dma_start(
-                out=out[first * P:(first + lower) * P, j * P:(j + 1) * P].rearrange("(a i) c -> i a c", i=P),
-                in_=m_view(j, hh)[:, 0:lower * P].rearrange("p (a c) -> p a c", c=P))
-
-
-        for op in LOADS:
-            if op[0] == "z":
-                e_zld("D", op[1])
-            elif op[0] == "x":
-                e_xld("D", op[1])
-            else:
-                e_wld("D", op[1])
-
-        def heads_of(z):
+        def half_row(z):
             return z // 2, (2 * (z % 2), 2 * (z % 2) + 1)
 
-        def z_squares(z):
-            zi, hs = heads_of(z)
-            for h in hs:
-                e_zsq("S", zi, h)
+        def transpose_z(z):
+            i, heads = half_row(z)
+            for h in heads:
+                transpose_words(("z", i, h), z_rows[i][:, h, :])
+
+        def copy_z(i, h):
+            if i not in z_groups:
+                z_groups[i] = zg_pool.tile([P, 4, 2, P, 4], BF16, name="z_group", align_bytes=64)
+            words_side_by_side("vector", z_groups[i][:, h], ("z", i, h))
+
+        def transpose_and_copy_z(z):
+            i, heads = half_row(z)
+            for h in heads:
+                transpose_words(("z", i, h), z_rows[i][:, h, :])
+                copy_z(i, h)
+
+        def quantise_z(i):
+            nc.vector.quantize_mx(out=z_words[:, i, :].bitcast(FP8X4), scales=z_scales[:, i, :],
+                                  in_=z_groups[i][:].rearrange("p h g n t -> p (h g n t)"))
+
+        def square_z(z):
+            i, heads = half_row(z)
+            for h in heads:
+                nc.scalar.activation(out=scratch(), in_=z_rows[i][:, h, :], func=ACT.Square,
+                                     accum_out=z_sq[:, 4 * i + h:4 * i + h + 1])
             if z % 2 == 1:
-                e_zpow("G", zi)
+                c = slice(4 * i, 4 * i + 4)
+                nc.gpsimd.tensor_tensor(out=z_norm[:, c], in0=z_sq[:, c], in1=half[:, 0:4], op=ALU.pow)
+                nc.gpsimd.tensor_scalar(out=z_norm_eps[:, c], in0=z_norm[:, c], scalar1=EPS, scalar2=1.0,
+                                        op0=ALU.add, op1=ALU.mult)
+                nc.gpsimd.tensor_tensor(out=rz[:, c], in0=z_norm_eps[:, c], in1=minus_one[:, 0:4], op=ALU.pow)
 
-        def z_turn(z):
-            zi, hs = heads_of(z)
-            for h in hs:
-                e_ztr("PE", zi, h)
-                e_zcp("S" if z >= ZSW else "V", zi, h)
+        def prepare_x(first_tile):
+            hf = first_tile // 4
+            for m in range(first_tile, first_tile + 4):
+                transpose_words(("x", m), x_rows[:, m, :])
+                if hf not in x_groups:
+                    x_groups[hf] = group_pool.tile([P, 4, 2, P, 4], BF16, name="x_group", tag="groups", align_bytes=64)
+                words_side_by_side("vector", x_groups[hf][:, m % 4], ("x", m))
+            tiles = slice(first_tile, first_tile + 4)
+            nc.vector.quantize_mx(out=x_words[:, tiles, :].rearrange("p a b -> p (a b)").bitcast(FP8X4),
+                                  scales=x_scales[:, tiles, :].rearrange("p a b -> p (a b)"),
+                                  in_=x_groups[hf][:].rearrange("p j g n t -> p (j g n t)"))
 
-        def z_ahead(z):
-            zi, hs = heads_of(z)
-            for h in hs:
-                e_ztr("PE", zi, h)
+        def regroup_w(engine, g, a):
+            if g not in w_groups:
+                w_groups[g] = group_pool.tile([P, 1024, 4], BF16, name="w_group", tag="groups", align_bytes=64)
+            copy(engine, w_groups[g][:, 256 * a:256 * (a + 1), :].rearrange("p (f q) t -> p f q t", f=2),
+                 w_rows[:, g, :, 256 * a:256 * (a + 1)].rearrange("p t (q f) -> p f q t", f=2))
 
-        def z_close(zi):
-            e_zq("V", zi)
-            e_rzv("V", zi)
+        def quantise_w(g, c):
+            cols = slice(512 * c, 512 * (c + 1))
+            nc.vector.quantize_mx(out=w_words[:, g, cols].bitcast(FP8X4), scales=w_scales[:, g, cols],
+                                  in_=w_groups[g][:, cols, :].rearrange("p c t -> p (c t)"))
 
-        def x_square(mt, eh):
-            e_s1n("PE", mt, eh)
-            e_xsq("S", mt, eh)
-
-        def fin1(u):
-            j, hh = u // 2, u % 2
-            if 0 <= u < 16 and span(j, hh)[1] > 0:
-                e_ftr("PE", j, hh)
-                e_own(OWN if u < 14 else "V", j, hh)
-                e_sum("V", j, hh)
-
-        def fin_ln(u):
-            if 0 <= u < 16 and span(u // 2, u % 2)[1] > 0:
-                e_ln("S", u // 2, u % 2)
-
-        def fin_ex(u):
-            if span(u // 2, u % 2)[1] > 0:
-                e_ex("S", u // 2, u % 2)
-                e_st("D", u // 2, u % 2)
-
-        def fin_mirror(u, who):
-            j, hh = u // 2, u % 2
-            if lower_of(j, hh)[1] > 0:
-                e_mtr("PE", j, hh)
-                e_mcp(who, j, hh)
-                e_mst("D", j, hh)
-
-        def xe_half(hf):
+        def x_emb_transposed(first_tile):
             for big in range(2):
-                for ms in range(4 * hf, 4 * hf + 4):
-                    e_s1t("PE", ms, big)
-                    e_xecp(XECP[hf][ms % 2], ms, big)
+                for m in range(first_tile, first_tile + 4):
+                    acc = bank("mx", [P, 4, P])
+                    for t in range(4):
+                        col = (4 * big + t) * P
+                        for g in range(2):
+                            nc.tensor.matmul_mx(out=acc[:, t, :],
+                                                lhsT=w_words[:, g, col:col + P].bitcast(FP8X4),
+                                                lhsT_scale=w_scales[:, g, col:col + P],
+                                                rhs=x_words[:, m, g * P:(g + 1) * P].bitcast(FP8X4),
+                                                rhs_scale=x_scales[:, m, g * P:(g + 1) * P],
+                                                start=(g == 0), stop=(g == 1))
+                    copy("vector", xe_groups[:, big, m * P:(m + 1) * P, :], acc[:].rearrange("p t m -> p m t"))
 
-        def x_half(hf):
-            for m in range(4 * hf, 4 * hf + 4):
-                e_xtr("PE", m)
-                e_xcp(XCP[hf][m % 2], m)
-            e_xq("V", hf)
+        def quantise_x_emb(c):
+            cols = slice(512 * c, 512 * (c + 1))
+            for big in range(2):
+                nc.vector.quantize_mx(out=xe_words[:, big, cols].bitcast(FP8X4), scales=xe_scales[:, big, cols],
+                                      in_=xe_groups[:, big, cols, :].rearrange("p m t -> p (m t)"))
 
-        x_half(0)
+        def square_x_emb(m, c):
+            cols = slice(512 * c, 512 * (c + 1))
+            acc = bank("mx", [P, 512])
+            for g in range(2):
+                nc.tensor.matmul_mx(out=acc[:],
+                                    lhsT=x_words[:, m, g * P:(g + 1) * P].bitcast(FP8X4),
+                                    lhsT_scale=x_scales[:, m, g * P:(g + 1) * P],
+                                    rhs=w_words[:, g, cols].bitcast(FP8X4), rhs_scale=w_scales[:, g, cols],
+                                    start=(g == 0), stop=(g == 1))
+            nc.scalar.activation(out=scratch()[:, 0:512], in_=acc[:], func=ACT.Square,
+                                 accum_out=x_sq_halves[:, 2 * m + c:2 * m + c + 1])
+
+        def x_norms():
+            pairs = x_sq_halves[:].rearrange("p (m c) -> p m c", c=2)
+            nc.gpsimd.tensor_tensor(out=x_sq[:], in0=pairs[:, :, 0], in1=pairs[:, :, 1], op=ALU.add)
+            nc.gpsimd.tensor_tensor(out=x_norm[:], in0=x_sq[:], in1=half[:], op=ALU.pow)
+            nc.gpsimd.tensor_scalar(out=x_norm_eps[:], in0=x_norm[:], scalar1=EPS, scalar2=1.0,
+                                    op0=ALU.add, op1=ALU.mult)
+            nc.gpsimd.tensor_tensor(out=rx[:], in0=x_norm_eps[:], in1=minus_one[:], op=ALU.pow)
+
+        def spread_rx(c):
+            row = bank("tr", [P, 512])
+            for j in range(4):
+                m = 4 * c + j
+                nc.tensor.matmul(out=row[:, j * P:(j + 1) * P], lhsT=rx[:, m:m + 1].to_broadcast([P, P]),
+                                 rhs=ident[:], start=True, stop=True)
+            copy("scalar", rx_row[:, 512 * c:512 * (c + 1)], row[:])
+
+        def multiply(s, h):
+            i, c = s // 2, s % 2
+            cols = slice(512 * c, 512 * (c + 1))
+            banks[("aff", s, h)] = bank("mx", [P, 512])
+            for big in range(2):
+                col = (2 * h + big) * P
+                nc.tensor.matmul_mx(out=banks[("aff", s, h)][:],
+                                    lhsT=z_words[:, i, col:col + P].bitcast(FP8X4),
+                                    lhsT_scale=z_scales[:, i, col:col + P],
+                                    rhs=xe_words[:, big, cols].bitcast(FP8X4), rhs_scale=xe_scales[:, big, cols],
+                                    start=(big == 0), stop=(big == 1))
+
+        def work(index):
+            if "work" not in late:
+                late["work"] = shared.tile([P, 8, 512], F32, name="work", tag="slot_c", align_bytes=64)
+            return late["work"][:, index, :]
+
+        def take_head(s, h, first_on_scalar):
+            i, c = s // 2, s % 2
+            acc = banks[("aff", s, h)]
+            scale = rz[:, 4 * i + h:4 * i + h + 1]
+            base = 2 * (s % 2)
+            if h == 0:
+                if first_on_scalar:
+                    nc.scalar.activation(out=work(base), in_=acc[:], func=ACT.Copy, scale=scale)
+                else:
+                    nc.vector.tensor_scalar_mul(out=work(base), in0=acc[:], scalar1=scale)
+                return
+            if h == 3:
+                if i not in b:
+                    four_rows = shared.tile([P, 4, 1024], F32, name="four_rows", tag="slot_a" if i < 4 else "slot_b")
+                    for k in range(4):
+                        b[4 * (i // 4) + k] = four_rows[:, k, :]
+                dst = b[i][:, 512 * c:512 * (c + 1)]
+            else:
+                dst = work(base + h % 2)
+            nc.vector.scalar_tensor_tensor(out=dst, in0=acc[:], scalar=scale, in1=work(base + (h - 1) % 2),
+                                           op0=ALU.mult, op1=ALU.max)
+
+        with_blocks = [s for s in range(16) if blocks_of(s)[1] > 0]
+        with_mirror = [s for s in range(16) if min(blocks_of(s)[1], s // 2 - blocks_of(s)[0]) > 0]
+
+        def result(s):
+            n = with_blocks.index(s)
+            if ("result", n // 4) not in late:
+                late[("result", n // 4)] = group_pool.tile([P, 4, 512], F32, name="results", tag="groups",
+                                                           align_bytes=64)
+            return late[("result", n // 4)][:, n % 4, :]
+
+        def add_up(s, own_engine):
+            first, count = blocks_of(s)
+            if count == 0:
+                return
+            j, width = s // 2, count * P
+            turned = bank("tr", [P, 4, P])
+            for k in range(count):
+                nc.tensor.transpose(turned[:, k, :], b[first + k][:, j * P:(j + 1) * P], ident[:])
+            cols = slice(P * first, P * first + width)
+            own = work(4 + with_blocks.index(s) % 4)[:, 0:width]
+            if own_engine == "vector":
+                nc.vector.tensor_tensor(out=own, in0=b[j][:, cols], in1=rx_row[:, cols], op=ALU.mult)
+            else:
+                nc.gpsimd.tensor_tensor(out=own, in0=b[j][:, cols], in1=rx_row[:, cols], op=ALU.mult)
+            nc.vector.scalar_tensor_tensor(out=result(s)[:, 0:width],
+                                           in0=turned[:].rearrange("p a b -> p (a b)")[:, 0:width],
+                                           scalar=rx[:, j:j + 1], in1=own, op0=ALU.mult, op1=ALU.add)
+
+        def logarithm(s):
+            width = blocks_of(s)[1] * P
+            if width > 0:
+                nc.scalar.activation(out=result(s)[:, 0:width], in_=result(s)[:, 0:width], func=ACT.Ln,
+                                     bias=0.5, scale=0.25)
+
+        def power_and_store(s):
+            first, count = blocks_of(s)
+            if count == 0:
+                return
+            j, width = s // 2, count * P
+            nc.scalar.activation(out=result(s)[:, 0:width], in_=result(s)[:, 0:width], func=ACT.Exp,
+                                 scale=beta_f[:, 0:1])
+            nc.sync.dma_start(out=out[j * P:(j + 1) * P, P * first:P * first + width], in_=result(s)[:, 0:width])
+
+        def mirror(s, engine):
+            if s not in with_mirror:
+                return
+            first, count = blocks_of(s)
+            j = s // 2
+            below = min(count, j - first)
+            turned = bank("tr", [P, 4, P])
+            for k in range(below):
+                nc.tensor.transpose(turned[:, k, :], result(s)[:, k * P:(k + 1) * P], ident[:])
+            n = with_mirror.index(s)
+            if ("mirror", n // 4) not in late:
+                late[("mirror", n // 4)] = z_pool.tile([P, 4, 512], F32, name="z_tile")
+            above = late[("mirror", n // 4)][:, n % 4, 0:below * P]
+            copy(engine, above, turned[:].rearrange("p a b -> p (a b)")[:, 0:below * P])
+            nc.sync.dma_start(
+                out=out[first * P:(first + below) * P, j * P:(j + 1) * P].rearrange("(a i) c -> i a c", i=P),
+                in_=above.rearrange("p (a c) -> p a c", c=P))
+
+        for m in range(4):
+            load_x_tile(m)
+        for a in range(4):
+            load_w_quarter(a)
+        load_z(0)
+        load_x_second_half()
+        for i in range(1, Z_BUFFERS):
+            load_z(i)
+
+        prepare_x(0)
         for g in range(2):
-            for a in range(4):
-                e_wre(WRE[a], g, a)
+            for a, engine in enumerate(("gpsimd", "scalar", "vector", "scalar")):
+                regroup_w(engine, g, a)
         for c in range(2):
             for g in range(2):
-                e_wq("V", g, c)
-        z_squares(0)
-        z_squares(1)
-        xe_half(0)
-        z_turn(0)
-        x_half(1)
-        for big in range(2):
-            e_xeq("V", big, 0)
-        for mt in range(NSQ0):
-            x_square(mt, 0)
-            x_square(mt, 1)
-        z_turn(1)
-        e_zld("D", 7)
-        z_squares(2)
-        z_squares(3)
-        xe_half(1)
-        z_close(0)
-        z_turn(2)
-        for big in range(2):
-            e_xeq("V", big, 1)
-        z_turn(3)
-        for z in range(4, ZSQ0):
-            z_squares(z)
+                quantise_w(g, c)
+        square_z(0)
+        square_z(1)
+        x_emb_transposed(0)
+        transpose_and_copy_z(0)
+        prepare_x(4)
+        quantise_x_emb(0)
+        for m in range(4):
+            square_x_emb(m, 0)
+            square_x_emb(m, 1)
+        transpose_and_copy_z(1)
+        load_z(7)
+        square_z(2)
+        square_z(3)
+        x_emb_transposed(4)
+        quantise_z(0)
+        transpose_and_copy_z(2)
+        quantise_x_emb(1)
+        transpose_and_copy_z(3)
+        square_z(4)
+        square_z(5)
 
-        fin_from = 2 * (8 - NSQ0) + 3
-        z_ahead(4)
+        transpose_z(4)
         for s in range(16):
-            i, hh = s // 2, s % 2
-            for c in PEO:
-                if c in "0123":
-                    e_umm("PE", i, hh, int(c))
-                elif s + 5 < 16:
-                    zi, hs = heads_of(s + 5)
-                    e_ztr("PE", zi, hs[0 if c == "a" else 1])
+            for h in range(4):
+                multiply(s, h)
+            if s + 5 < 16:
+                transpose_z(s + 5)
             between = []
             if s + 4 < 16:
-                zi, hs = heads_of(s + 4)
-                for h in hs:
-                    if s + 4 >= ZSW or (h % 2 == 1 and ZS1[0] <= s < ZS1[1]):
-                        e_zcp("S", zi, h)
-                    else:
-                        between.append(("zcp", zi, h))
-            if s > fin_from:
-                between.append(("fin", s - 1, 0))
-            if s + 3 < 16 and (s + 3) % 2 == 1:
-                between.append(("close", (s + 3) // 2, 0))
+                i, heads = half_row(s + 4)
+                between.append(lambda i=i, h=heads[0]: copy_z(i, h))
+                between.append(lambda i=i, h=heads[1]: copy_z(i, h))
+            if s > SUMS_FROM:
+                between.append(lambda s=s: add_up(s - 1, "gpsimd" if s - 1 < 14 else "vector"))
+            if s % 2 == 0 and s + 3 < 16:
+                between.append(lambda s=s: quantise_z((s + 3) // 2))
             for h in range(4):
-                e_ev("S" if (h == 0 and EVS[0] <= s < EVS[1]) else "V", i, hh, h)
-                if h >= 1 and h - 1 < len(between):
-                    job = between[h - 1]
-                    if job[0] == "zcp":
-                        e_zcp("V", job[1], job[2])
-                    elif job[0] == "fin":
-                        fin1(job[1])
-                    else:
-                        z_close(job[1])
-            if s + ZSQ0 < 16:
-                z_squares(s + ZSQ0)
-            if s < 2 * (8 - NSQ0):
-                x_square(NSQ0 + s // 2, s % 2)
-            if s == 8:
+                take_head(s, h, first_on_scalar=(s < FIRST_BATCH))
+                if 1 <= h <= len(between):
+                    between[h - 1]()
+            if s + 6 < 16:
+                square_z(s + 6)
+            if s < 8:
+                square_x_emb(4 + s // 2, s % 2)
+            if s == SUMS_FROM - 3:
                 nc.gpsimd.tensor_copy(out=beta_f[:], in_=beta_bf[:])
-            if s == fin_from - 3:
-                e_xn1("V")
-                e_xpow("G")
-            if s == fin_from - 2:
-                e_rxv("V")
-            if s == fin_from - 1:
-                for k in range(2):
-                    e_spr("PE", k)
-                    e_spc("S", k)
-            if s == fin_from:
-                for u in range(s):
-                    fin1(u)
-                for u in range(s - 1):
-                    fin_ln(u)
-            if s > fin_from and s <= 12:
-                fin_ln(s - 2)
-            if s == 12:
-                fin_ln(11)
-                for u in range(8):
-                    fin_ex(u)
-            if s == 13:
-                for u in range(8, 12):
-                    fin_ex(u)
-                for u in range(8):
-                    fin_mirror(u, "S")
-            if s == 14:
-                for u in range(8, 12):
-                    fin_mirror(u, "S")
-                fin_ln(12)
-                fin_ln(13)
-            if s == 15:
-                fin_ln(14)
-        fin1(15)
-        fin_ln(15)
-        for u in range(12, 16):
-            fin_ex(u)
-        for u in range(12, 16):
-            fin_mirror(u, "V")
+                x_norms()
+            if s == SUMS_FROM - 1:
+                spread_rx(0)
+                spread_rx(1)
+            if s == SUMS_FROM:
+                for earlier in range(s):
+                    add_up(earlier, "gpsimd")
+                for earlier in range(s - 1):
+                    logarithm(earlier)
+            if s == FIRST_BATCH:
+                logarithm(s - 2)
+                logarithm(s - 1)
+                for earlier in range(8):
+                    power_and_store(earlier)
+            if s == FIRST_BATCH + 1:
+                for earlier in range(8, FIRST_BATCH):
+                    power_and_store(earlier)
+                for earlier in range(8):
+                    mirror(earlier, "scalar")
+            if s == FIRST_BATCH + 2:
+                for earlier in range(8, FIRST_BATCH):
+                    mirror(earlier, "scalar")
+                logarithm(FIRST_BATCH)
+                logarithm(FIRST_BATCH + 1)
+            if s == FIRST_BATCH + 3:
+                logarithm(FIRST_BATCH + 2)
+        add_up(15, "vector")
+        logarithm(15)
+        for s in range(FIRST_BATCH, 16):
+            power_and_store(s)
+        for s in range(FIRST_BATCH, 16):
+            mirror(s, "vector")

@@ -52,12 +52,10 @@ def tile_affnet_t_kernel(tc, X, W, Z, beta, out):
 
         ident = const.tile([P, P], F32)
         make_identity(nc, ident[:])
-        half = const.tile([P, 8], F32)
+        half = const.tile([P, 1], F32)
         nc.vector.memset(half[:], 0.5)
-        minus_one = const.tile([P, 8], F32)
-        nc.vector.memset(minus_one[:], -1.0)
         warm = const.tile([P, 1], F32)
-        nc.scalar.activation(out=warm[:], in_=half[:, 0:1], func=ACT.Ln)
+        nc.scalar.activation(out=warm[:], in_=half[:, 0:1], func=ACT.Sqrt)
         beta_bf = const.tile([P, 1], BF16)
         nc.scalar.dma_start(out=beta_bf[:], in_=beta.partition_broadcast(P))
         beta_f = const.tile([P, 1], F32)
@@ -151,12 +149,18 @@ def tile_affnet_t_kernel(tc, X, W, Z, beta, out):
             for h in heads:
                 nc.scalar.activation(out=scratch(), in_=z_rows[i][:, h, :], func=ACT.Square,
                                      accum_out=z_sq[:, 4 * i + h:4 * i + h + 1])
-            if z % 2 == 1:
-                c = slice(4 * i, 4 * i + 4)
-                nc.gpsimd.tensor_tensor(out=z_norm[:, c], in0=z_sq[:, c], in1=half[:, 0:4], op=ALU.pow)
-                nc.gpsimd.tensor_scalar(out=z_norm_eps[:, c], in0=z_norm[:, c], scalar1=EPS, scalar2=1.0,
-                                        op0=ALU.add, op1=ALU.mult)
-                nc.gpsimd.tensor_tensor(out=rz[:, c], in0=z_norm_eps[:, c], in1=minus_one[:, 0:4], op=ALU.pow)
+
+        def root_z(i):
+            c = slice(4 * i, 4 * i + 4)
+            nc.scalar.activation(out=z_norm[:, c], in_=z_sq[:, c], func=ACT.Sqrt)
+
+        def add_eps_z(i):
+            c = slice(4 * i, 4 * i + 4)
+            nc.scalar.activation(out=z_norm_eps[:, c], in_=z_norm[:, c], func=ACT.Copy, bias=EPS)
+
+        def invert_z(i):
+            c = slice(4 * i, 4 * i + 4)
+            nc.vector.reciprocal(out=rz[:, c], in_=z_norm_eps[:, c])
 
         def prepare_x(first_tile):
             hf = first_tile // 4
@@ -217,10 +221,8 @@ def tile_affnet_t_kernel(tc, X, W, Z, beta, out):
         def x_norms():
             pairs = x_sq_halves[:].rearrange("p (m c) -> p m c", c=2)
             nc.gpsimd.tensor_tensor(out=x_sq[:], in0=pairs[:, :, 0], in1=pairs[:, :, 1], op=ALU.add)
-            nc.gpsimd.tensor_tensor(out=x_norm[:], in0=x_sq[:], in1=half[:], op=ALU.pow)
-            nc.gpsimd.tensor_scalar(out=x_norm_eps[:], in0=x_norm[:], scalar1=EPS, scalar2=1.0,
-                                    op0=ALU.add, op1=ALU.mult)
-            nc.gpsimd.tensor_tensor(out=rx[:], in0=x_norm_eps[:], in1=minus_one[:], op=ALU.pow)
+            nc.scalar.activation(out=x_norm[:], in_=x_sq[:], func=ACT.Sqrt)
+            nc.scalar.activation(out=x_norm_eps[:], in_=x_norm[:], func=ACT.Copy, bias=EPS)
 
         def spread_rx(c):
             row = bank("tr", [P, 512])
@@ -357,15 +359,20 @@ def tile_affnet_t_kernel(tc, X, W, Z, beta, out):
             square_x_emb(m, 1)
         transpose_and_copy_z(1)
         load_z(7)
+        root_z(0)
         square_z(2)
+        add_eps_z(0)
         square_z(3)
         x_emb_transposed(4)
+        invert_z(0)
         quantise_z(0)
         transpose_and_copy_z(2)
         quantise_x_emb(1)
         transpose_and_copy_z(3)
         square_z(4)
+        root_z(1)
         square_z(5)
+        add_eps_z(1)
 
         transpose_z(4)
         for s in range(16):
@@ -384,15 +391,23 @@ def tile_affnet_t_kernel(tc, X, W, Z, beta, out):
                 between.append(lambda s=s: quantise_z((s + 3) // 2))
             for h in range(4):
                 take_head(s, h, first_on_scalar=(s < FIRST_BATCH))
+                if h == 0 and s % 2 == 0 and s // 2 + 2 < 8:
+                    root_z(s // 2 + 2)
+                if h == 0 and s % 2 == 1 and s // 2 + 1 < 8:
+                    invert_z(s // 2 + 1)
                 if 1 <= h <= len(between):
                     between[h - 1]()
             if s + 6 < 16:
                 square_z(s + 6)
+            if s % 2 == 0 and s // 2 + 2 < 8:
+                add_eps_z(s // 2 + 2)
             if s < 8:
                 square_x_emb(4 + s // 2, s % 2)
             if s == SUMS_FROM - 3:
                 nc.gpsimd.tensor_copy(out=beta_f[:], in_=beta_bf[:])
                 x_norms()
+            if s == SUMS_FROM - 2:
+                nc.vector.reciprocal(out=rx[:], in_=x_norm_eps[:])
             if s == SUMS_FROM - 1:
                 spread_rx(0)
                 spread_rx(1)

@@ -16,7 +16,21 @@ P = 128
 EPS = 1e-6
 BANKS = 4
 Z_BUFFERS = 7
-SUMS_FROM = 11
+RX_AT = 7
+LA = 4
+EARLY = 7
+ZC_A = {10, 11}
+ZC_B = set(range(12))
+OWN = {10: [0, 2, 4, 6, 8, 9], 11: [10], 12: [11], 13: [12], 14: [13]}
+FINISH = {10: [0, 2], 11: [4, 6], 12: [8, 9, 10], 13: [11], 14: [12], 15: []}
+FSLOT = {10: [3, 4], 11: [3, 4], 12: [1, 2, 4], 13: [2], 14: [2], 15: []}
+LOGS = {12: [0, 2, 4, 6], 13: [8, 9, 10, 11]}
+POWERS = {14: [0, 2, 4, 6, 8, 9, 10, 11]}
+X_ON_S = {2, 3, 7}
+XE_ON_S = {(2, 0), (3, 0), (2, 1), (3, 1)}
+H0_ON_V = set(range(16))
+XX_FIRST = 6
+XX_PRO = 9
 FIRST_BATCH = 12
 
 
@@ -83,7 +97,7 @@ def tile_affnet_t_kernel(tc, X, W, Z, beta, out):
         rx = keep.tile([P, 8], F32)
         rx_row = keep.tile([P, 1024], F32)
         x_rows = shared.tile([P, 8, 1024], BF16, name="x_rows", tag="slot_a")
-        w_rows = shared.tile([P, 2, 4, 1024], BF16, name="w_rows", tag="slot_b")
+        w_rows = shared.tile([P, 2, 2, 4, 512], BF16, name="w_rows", tag="slot_b")
         x_words = shared.tile([P, 8, 256], U32, align_bytes=64)
         x_scales = shared.tile([P, 8, 256], U8, align_bytes=64)
         w_words = shared.tile([P, 2, 1024], U32, align_bytes=64)
@@ -104,9 +118,10 @@ def tile_affnet_t_kernel(tc, X, W, Z, beta, out):
         def load_x_second_half():
             nc.sync.dma_start(out=x_rows[:, 4:8, :], in_=X[512:1024, :].rearrange("(t p) f -> p t f", p=P))
 
-        def load_w_quarter(a):
-            nc.sync.dma_start(out=w_rows[:, a // 2, 2 * (a % 2):2 * (a % 2) + 2, :],
-                              in_=W[256 * a:256 * (a + 1), :].rearrange("(p e) c -> p e c", e=2))
+        def load_w_piece(a, c):
+            cols = slice(512 * c, 512 * (c + 1))
+            nc.sync.dma_start(out=w_rows[:, c, a // 2, 2 * (a % 2):2 * (a % 2) + 2, :],
+                              in_=W[256 * a:256 * (a + 1), cols].rearrange("(p e) c -> p e c", e=2))
 
         def load_z(i):
             z_rows[i] = z_pool.tile([P, 4, 1024], BF16, name="z_tile")
@@ -129,10 +144,10 @@ def tile_affnet_t_kernel(tc, X, W, Z, beta, out):
             for h in heads:
                 transpose_words(("z", i, h), z_rows[i][:, h, :])
 
-        def copy_z(i, h):
+        def copy_z(i, h, engine="vector"):
             if i not in z_groups:
                 z_groups[i] = zg_pool.tile([P, 4, 2, P, 4], BF16, name="z_group", align_bytes=64)
-            words_side_by_side("vector", z_groups[i][:, h], ("z", i, h))
+            words_side_by_side(engine, z_groups[i][:, h], ("z", i, h))
 
         def transpose_and_copy_z(z):
             i, heads = half_row(z)
@@ -144,11 +159,14 @@ def tile_affnet_t_kernel(tc, X, W, Z, beta, out):
             nc.vector.quantize_mx(out=z_words[:, i, :].bitcast(FP8X4), scales=z_scales[:, i, :],
                                   in_=z_groups[i][:].rearrange("p h g n t -> p (h g n t)"))
 
+        def square_head(i, h):
+            nc.scalar.activation(out=scratch(), in_=z_rows[i][:, h, :], func=ACT.Square,
+                                 accum_out=z_sq[:, 4 * i + h:4 * i + h + 1])
+
         def square_z(z):
             i, heads = half_row(z)
             for h in heads:
-                nc.scalar.activation(out=scratch(), in_=z_rows[i][:, h, :], func=ACT.Square,
-                                     accum_out=z_sq[:, 4 * i + h:4 * i + h + 1])
+                square_head(i, h)
 
         def root_z(i):
             c = slice(4 * i, 4 * i + 4)
@@ -162,43 +180,45 @@ def tile_affnet_t_kernel(tc, X, W, Z, beta, out):
             c = slice(4 * i, 4 * i + 4)
             nc.vector.reciprocal(out=rz[:, c], in_=z_norm_eps[:, c])
 
-        def prepare_x(first_tile):
-            hf = first_tile // 4
-            for m in range(first_tile, first_tile + 4):
-                transpose_words(("x", m), x_rows[:, m, :])
-                if hf not in x_groups:
-                    x_groups[hf] = group_pool.tile([P, 4, 2, P, 4], BF16, name="x_group", tag="groups", align_bytes=64)
-                words_side_by_side("vector", x_groups[hf][:, m % 4], ("x", m))
-            tiles = slice(first_tile, first_tile + 4)
+        def turn_x(m):
+            transpose_words(("x", m), x_rows[:, m, :])
+
+        def copy_x(m):
+            if m // 4 not in x_groups:
+                x_groups[m // 4] = group_pool.tile([P, 4, 2, P, 4], BF16, name="x_group", tag="groups", align_bytes=64)
+            words_side_by_side("scalar" if m in X_ON_S else "vector", x_groups[m // 4][:, m % 4], ("x", m))
+
+        def quantise_x(first_tile, count):
+            tiles = slice(first_tile, first_tile + count)
+            inner = slice(first_tile % 4, first_tile % 4 + count)
             nc.vector.quantize_mx(out=x_words[:, tiles, :].rearrange("p a b -> p (a b)").bitcast(FP8X4),
                                   scales=x_scales[:, tiles, :].rearrange("p a b -> p (a b)"),
-                                  in_=x_groups[hf][:].rearrange("p j g n t -> p (j g n t)"))
+                                  in_=x_groups[first_tile // 4][:, inner].rearrange("p j g n t -> p (j g n t)"))
 
         def regroup_w(engine, g, a):
             if g not in w_groups:
                 w_groups[g] = group_pool.tile([P, 1024, 4], BF16, name="w_group", tag="groups", align_bytes=64)
             copy(engine, w_groups[g][:, 256 * a:256 * (a + 1), :].rearrange("p (f q) t -> p f q t", f=2),
-                 w_rows[:, g, :, 256 * a:256 * (a + 1)].rearrange("p t (q f) -> p f q t", f=2))
+                 w_rows[:, a // 2, g, :, 256 * (a % 2):256 * (a % 2 + 1)].rearrange("p t (q f) -> p f q t", f=2))
 
         def quantise_w(g, c):
             cols = slice(512 * c, 512 * (c + 1))
             nc.vector.quantize_mx(out=w_words[:, g, cols].bitcast(FP8X4), scales=w_scales[:, g, cols],
                                   in_=w_groups[g][:, cols, :].rearrange("p c t -> p (c t)"))
 
-        def x_emb_transposed(first_tile):
-            for big in range(2):
-                for m in range(first_tile, first_tile + 4):
-                    acc = bank("mx", [P, 4, P])
-                    for t in range(4):
-                        col = (4 * big + t) * P
-                        for g in range(2):
-                            nc.tensor.matmul_mx(out=acc[:, t, :],
-                                                lhsT=w_words[:, g, col:col + P].bitcast(FP8X4),
-                                                lhsT_scale=w_scales[:, g, col:col + P],
-                                                rhs=x_words[:, m, g * P:(g + 1) * P].bitcast(FP8X4),
-                                                rhs_scale=x_scales[:, m, g * P:(g + 1) * P],
-                                                start=(g == 0), stop=(g == 1))
-                    copy("vector", xe_groups[:, big, m * P:(m + 1) * P, :], acc[:].rearrange("p t m -> p m t"))
+        def x_emb_transposed(m, big):
+            acc = bank("mx", [P, 4, P])
+            for t in range(4):
+                col = (4 * big + t) * P
+                for g in range(2):
+                    nc.tensor.matmul_mx(out=acc[:, t, :],
+                                        lhsT=w_words[:, g, col:col + P].bitcast(FP8X4),
+                                        lhsT_scale=w_scales[:, g, col:col + P],
+                                        rhs=x_words[:, m, g * P:(g + 1) * P].bitcast(FP8X4),
+                                        rhs_scale=x_scales[:, m, g * P:(g + 1) * P],
+                                        start=(g == 0), stop=(g == 1))
+            copy("scalar" if (m, big) in XE_ON_S else "vector", xe_groups[:, big, m * P:(m + 1) * P, :],
+                 acc[:].rearrange("p t m -> p m t"))
 
         def quantise_x_emb(c):
             cols = slice(512 * c, 512 * (c + 1))
@@ -225,12 +245,13 @@ def tile_affnet_t_kernel(tc, X, W, Z, beta, out):
             nc.scalar.activation(out=x_norm_eps[:], in_=x_norm[:], func=ACT.Copy, bias=EPS)
 
         def spread_rx(c):
-            row = bank("tr", [P, 512])
+            banks[("row", c)] = bank("mx", [P, 512])
             for j in range(4):
                 m = 4 * c + j
-                nc.tensor.matmul(out=row[:, j * P:(j + 1) * P], lhsT=rx[:, m:m + 1].to_broadcast([P, P]),
-                                 rhs=ident[:], start=True, stop=True)
-            copy("scalar", rx_row[:, 512 * c:512 * (c + 1)], row[:])
+                nc.tensor.transpose(banks[("row", c)][:, j * P:(j + 1) * P], rx[:, m:m + 1].to_broadcast([P, P]), ident[:])
+
+        def keep_rx_row(c):
+            copy("scalar", rx_row[:, 512 * c:512 * (c + 1)], banks[("row", c)][:])
 
         def multiply(s, h):
             i, c = s // 2, s % 2
@@ -244,21 +265,35 @@ def tile_affnet_t_kernel(tc, X, W, Z, beta, out):
                                     rhs=xe_words[:, big, cols].bitcast(FP8X4), rhs_scale=xe_scales[:, big, cols],
                                     start=(big == 0), stop=(big == 1))
 
+        def multiply_half(s, h, part):
+            i, c = s // 2, s % 2
+            cols = slice(512 * c + 256 * part, 512 * c + 256 * (part + 1))
+            acc = bank("mx", [P, 256])
+            for big in range(2):
+                col = (2 * h + big) * P
+                nc.tensor.matmul_mx(out=acc[:],
+                                    lhsT=z_words[:, i, col:col + P].bitcast(FP8X4),
+                                    lhsT_scale=z_scales[:, i, col:col + P],
+                                    rhs=xe_words[:, big, cols].bitcast(FP8X4), rhs_scale=xe_scales[:, big, cols],
+                                    start=(big == 0), stop=(big == 1))
+            banks[("aff", s, h, part)] = acc
+
         def work(index):
             if "work" not in late:
                 late["work"] = shared.tile([P, 8, 512], F32, name="work", tag="slot_c", align_bytes=64)
             return late["work"][:, index, :]
 
-        def take_head(s, h, first_on_scalar):
+        def take_head(s, h, first_on_scalar, part=None):
             i, c = s // 2, s % 2
-            acc = banks[("aff", s, h)]
+            acc = banks[("aff", s, h)] if part is None else banks[("aff", s, h, part)]
             scale = rz[:, 4 * i + h:4 * i + h + 1]
             base = 2 * (s % 2)
+            some = slice(0, 512) if part is None else slice(256 * part, 256 * (part + 1))
             if h == 0:
                 if first_on_scalar:
-                    nc.scalar.activation(out=work(base), in_=acc[:], func=ACT.Copy, scale=scale)
+                    nc.scalar.activation(out=work(base)[:, some], in_=acc[:], func=ACT.Copy, scale=scale)
                 else:
-                    nc.vector.tensor_scalar_mul(out=work(base), in0=acc[:], scalar1=scale)
+                    nc.vector.tensor_scalar_mul(out=work(base)[:, some], in0=acc[:], scalar1=scale)
                 return
             if h == 3:
                 if i not in b:
@@ -268,7 +303,7 @@ def tile_affnet_t_kernel(tc, X, W, Z, beta, out):
                 dst = b[i][:, 512 * c:512 * (c + 1)]
             else:
                 dst = work(base + h % 2)
-            nc.vector.scalar_tensor_tensor(out=dst, in0=acc[:], scalar=scale, in1=work(base + (h - 1) % 2),
+            nc.vector.scalar_tensor_tensor(out=dst[:, some], in0=acc[:], scalar=scale, in1=work(base + (h - 1) % 2)[:, some],
                                            op0=ALU.mult, op1=ALU.max)
 
         with_blocks = [s for s in range(16) if blocks_of(s)[1] > 0]
@@ -281,161 +316,216 @@ def tile_affnet_t_kernel(tc, X, W, Z, beta, out):
                                                            align_bytes=64)
             return late[("result", n // 4)][:, n % 4, :]
 
-        def add_up(s, own_engine):
+        def first_term(s, engine, lo=0, hi=4):
             first, count = blocks_of(s)
-            if count == 0:
-                return
-            j, width = s // 2, count * P
-            turned = bank("tr", [P, 4, P])
-            for k in range(count):
-                nc.tensor.transpose(turned[:, k, :], b[first + k][:, j * P:(j + 1) * P], ident[:])
-            cols = slice(P * first, P * first + width)
-            own = work(4 + with_blocks.index(s) % 4)[:, 0:width]
-            if own_engine == "vector":
-                nc.vector.tensor_tensor(out=own, in0=b[j][:, cols], in1=rx_row[:, cols], op=ALU.mult)
-            else:
-                nc.gpsimd.tensor_tensor(out=own, in0=b[j][:, cols], in1=rx_row[:, cols], op=ALU.mult)
-            nc.vector.scalar_tensor_tensor(out=result(s)[:, 0:width],
-                                           in0=turned[:].rearrange("p a b -> p (a b)")[:, 0:width],
-                                           scalar=rx[:, j:j + 1], in1=own, op0=ALU.mult, op1=ALU.add)
+            j, part = s // 2, slice(lo * P, min(hi, count) * P)
+            cols = slice(P * first + part.start, P * first + part.stop)
+            engine.tensor_tensor(out=result(s)[:, part], in0=b[j][:, cols], in1=rx_row[:, cols], op=ALU.mult)
 
-        def logarithm(s):
-            width = blocks_of(s)[1] * P
-            if width > 0:
-                nc.scalar.activation(out=result(s)[:, 0:width], in_=result(s)[:, 0:width], func=ACT.Ln,
-                                     bias=0.5, scale=0.25)
-
-        def power_and_store(s):
-            first, count = blocks_of(s)
-            if count == 0:
-                return
-            j, width = s // 2, count * P
-            nc.scalar.activation(out=result(s)[:, 0:width], in_=result(s)[:, 0:width], func=ACT.Exp,
-                                 scale=beta_f[:, 0:1])
-            nc.sync.dma_start(out=out[j * P:(j + 1) * P, P * first:P * first + width], in_=result(s)[:, 0:width])
-
-        def mirror(s, engine):
-            if s not in with_mirror:
-                return
+        def turn(s, lo=0, hi=4):
             first, count = blocks_of(s)
             j = s // 2
-            below = min(count, j - first)
+            banks[("turned", s, lo)] = bank("tr", [P, 4, P])
+            for k in range(lo, min(hi, count)):
+                nc.tensor.transpose(banks[("turned", s, lo)][:, k, :], b[first + k][:, j * P:(j + 1) * P], ident[:])
+
+        def add_second_term(s, lo=0, hi=4):
+            first, count = blocks_of(s)
+            j, part = s // 2, slice(lo * P, min(hi, count) * P)
+            nc.vector.scalar_tensor_tensor(out=result(s)[:, part],
+                                           in0=banks[("turned", s, lo)][:].rearrange("p a b -> p (a b)")[:, part],
+                                           scalar=rx[:, j:j + 1], in1=result(s)[:, part],
+                                           op0=ALU.mult, op1=ALU.add)
+
+        def logarithm(s, lo=0, hi=4):
+            part = slice(lo * P, min(hi, blocks_of(s)[1]) * P)
+            nc.scalar.activation(out=result(s)[:, part], in_=result(s)[:, part], func=ACT.Ln, bias=0.5, scale=0.25)
+
+        def power_and_store(s, lo=0, hi=4):
+            first, count = blocks_of(s)
+            j, part = s // 2, slice(lo * P, min(hi, count) * P)
+            nc.scalar.activation(out=result(s)[:, part], in_=result(s)[:, part], func=ACT.Exp, scale=beta_f[:, 0:1])
+            nc.sync.dma_start(out=out[j * P:(j + 1) * P, P * first + part.start:P * first + part.stop],
+                              in_=result(s)[:, part])
+
+        def mirror(s, engine, lo=0, hi=4):
+            first, count = blocks_of(s)
+            j = s // 2
+            hi = min(hi, count, j - first)
             turned = bank("tr", [P, 4, P])
-            for k in range(below):
+            for k in range(lo, hi):
                 nc.tensor.transpose(turned[:, k, :], result(s)[:, k * P:(k + 1) * P], ident[:])
             n = with_mirror.index(s)
             if ("mirror", n // 4) not in late:
                 late[("mirror", n // 4)] = z_pool.tile([P, 4, 512], F32, name="z_tile")
-            above = late[("mirror", n // 4)][:, n % 4, 0:below * P]
-            copy(engine, above, turned[:].rearrange("p a b -> p (a b)")[:, 0:below * P])
+            above = late[("mirror", n // 4)][:, n % 4, lo * P:hi * P]
+            copy(engine, above, turned[:].rearrange("p a b -> p (a b)")[:, lo * P:hi * P])
             nc.sync.dma_start(
-                out=out[first * P:(first + below) * P, j * P:(j + 1) * P].rearrange("(a i) c -> i a c", i=P),
+                out=out[(first + lo) * P:(first + hi) * P, j * P:(j + 1) * P].rearrange("(a i) c -> i a c", i=P),
                 in_=above.rearrange("p (a c) -> p a c", c=P))
 
-        for m in range(4):
-            load_x_tile(m)
+        load_x_tile(0)
+        load_x_tile(1)
         for a in range(4):
-            load_w_quarter(a)
+            load_w_piece(a, 0)
+        load_x_tile(2)
+        load_x_tile(3)
+        for a in range(4):
+            load_w_piece(a, 1)
         load_z(0)
         load_x_second_half()
         for i in range(1, Z_BUFFERS):
             load_z(i)
 
-        prepare_x(0)
-        for g in range(2):
-            for a, engine in enumerate(("gpsimd", "scalar", "vector", "scalar")):
-                regroup_w(engine, g, a)
-        for c in range(2):
-            for g in range(2):
-                quantise_w(g, c)
-        square_z(0)
-        square_z(1)
-        x_emb_transposed(0)
-        transpose_and_copy_z(0)
-        prepare_x(4)
-        quantise_x_emb(0)
+        turn_x(0)
+        turn_x(1)
+        copy_x(0)
+        copy_x(1)
+        quantise_x(0, 2)
+        regroup_w("vector", 0, 0)
+        regroup_w("scalar", 0, 1)
+        regroup_w("vector", 1, 0)
+        regroup_w("scalar", 1, 1)
+        turn_x(2)
+        turn_x(3)
+        quantise_w(0, 0)
+        copy_x(2)
+        quantise_w(1, 0)
+        copy_x(3)
+        quantise_x(2, 2)
+        regroup_w("gpsimd", 0, 2)
+        regroup_w("scalar", 0, 3)
+        for m in range(2):
+            x_emb_transposed(m, 0)
+        regroup_w("vector", 1, 2)
+        regroup_w("scalar", 1, 3)
+        for m in range(2, 4):
+            x_emb_transposed(m, 0)
+        quantise_w(0, 1)
+        quantise_w(1, 1)
+        square_head(0, 0)
         for m in range(4):
-            square_x_emb(m, 0)
-            square_x_emb(m, 1)
+            x_emb_transposed(m, 1)
+        square_head(0, 1)
+        for m in range(4, 8):
+            turn_x(m)
+            copy_x(m)
+        transpose_and_copy_z(0)
+        quantise_x(4, 4)
+        quantise_x_emb(0)
+        for u in range(XX_FIRST):
+            square_x_emb(u // 2, u % 2)
         transpose_and_copy_z(1)
+        for m in range(4, 8):
+            x_emb_transposed(m, 0)
+        square_head(0, 2)
+        square_head(0, 3)
+        for m in range(4, 8):
+            x_emb_transposed(m, 1)
         load_z(7)
         root_z(0)
-        square_z(2)
+        for u in range(XX_FIRST, XX_PRO):
+            square_x_emb(u // 2, u % 2)
         add_eps_z(0)
-        square_z(3)
-        x_emb_transposed(4)
-        invert_z(0)
         quantise_z(0)
         transpose_and_copy_z(2)
+        invert_z(0)
         quantise_x_emb(1)
         transpose_and_copy_z(3)
-        square_z(4)
-        root_z(1)
-        square_z(5)
-        add_eps_z(1)
+        for z in range(2, LA):
+            square_z(z)
+        if LA > 3:
+            root_z(1)
+            add_eps_z(1)
 
         transpose_z(4)
-        for s in range(16):
+        for s in range(15):
             for h in range(4):
                 multiply(s, h)
             if s + 5 < 16:
                 transpose_z(s + 5)
-            between = []
+            between = [[], [], [], [], []]
             if s + 4 < 16:
                 i, heads = half_row(s + 4)
-                between.append(lambda i=i, h=heads[0]: copy_z(i, h))
-                between.append(lambda i=i, h=heads[1]: copy_z(i, h))
-            if s > SUMS_FROM:
-                between.append(lambda s=s: add_up(s - 1, "gpsimd" if s - 1 < 14 else "vector"))
+                between[1].append(lambda i=i, h=heads[0]: copy_z(i, h, "scalar" if s in ZC_A else "vector"))
+                between[2].append(lambda i=i, h=heads[1]: copy_z(i, h, "scalar" if s in ZC_B else "vector"))
+            for n, k in enumerate(FINISH.get(s, [])):
+                between[FSLOT[s][n]].append(lambda k=k: add_second_term(k))
             if s % 2 == 0 and s + 3 < 16:
-                between.append(lambda s=s: quantise_z((s + 3) // 2))
+                between[3].append(lambda s=s: quantise_z((s + 3) // 2))
+            for k in OWN.get(s, []):
+                first_term(k, nc.gpsimd)
             for h in range(4):
-                take_head(s, h, first_on_scalar=(s < FIRST_BATCH))
-                if h == 0 and s % 2 == 0 and s // 2 + 2 < 8:
-                    root_z(s // 2 + 2)
-                if h == 0 and s % 2 == 1 and s // 2 + 1 < 8:
+                take_head(s, h, first_on_scalar=s not in H0_ON_V)
+                if h == 0 and s % 2 == LA % 2 and (2 if LA > 3 else 1) <= (s + LA - 2) // 2 < EARLY:
+                    root_z((s + LA - 2) // 2)
+                if h == (0 if LA > 3 else 3) and s % 2 == 1 and s // 2 + 1 < 8:
                     invert_z(s // 2 + 1)
-                if 1 <= h <= len(between):
-                    between[h - 1]()
-            if s + 6 < 16:
-                square_z(s + 6)
-            if s % 2 == 0 and s // 2 + 2 < 8:
-                add_eps_z(s // 2 + 2)
-            if s < 8:
-                square_x_emb(4 + s // 2, s % 2)
-            if s == SUMS_FROM - 3:
-                nc.gpsimd.tensor_copy(out=beta_f[:], in_=beta_bf[:])
-                x_norms()
-            if s == SUMS_FROM - 2:
-                nc.vector.reciprocal(out=rx[:], in_=x_norm_eps[:])
-            if s == SUMS_FROM - 1:
+                if h == (3 if s < 12 else 0):
+                    for k in FINISH.get(s, []):
+                        turn(k)
+                for piece in between[h]:
+                    piece()
+            for piece in between[4]:
+                piece()
+            if s == RX_AT + 2:
                 spread_rx(0)
                 spread_rx(1)
-            if s == SUMS_FROM:
-                for earlier in range(s):
-                    add_up(earlier, "gpsimd")
-                for earlier in range(s - 1):
-                    logarithm(earlier)
-            if s == FIRST_BATCH:
-                logarithm(s - 2)
-                logarithm(s - 1)
-                for earlier in range(8):
-                    power_and_store(earlier)
-            if s == FIRST_BATCH + 1:
-                for earlier in range(8, FIRST_BATCH):
-                    power_and_store(earlier)
-                for earlier in range(8):
-                    mirror(earlier, "scalar")
-            if s == FIRST_BATCH + 2:
-                for earlier in range(8, FIRST_BATCH):
-                    mirror(earlier, "scalar")
-                logarithm(FIRST_BATCH)
-                logarithm(FIRST_BATCH + 1)
-            if s == FIRST_BATCH + 3:
-                logarithm(FIRST_BATCH + 2)
-        add_up(15, "vector")
-        logarithm(15)
-        for s in range(FIRST_BATCH, 16):
-            power_and_store(s)
-        for s in range(FIRST_BATCH, 16):
-            mirror(s, "vector")
+            if s + LA < 16:
+                square_z(s + LA)
+            if s % 2 == LA % 2 and (2 if LA > 3 else 1) <= (s + LA - 2) // 2 < EARLY:
+                add_eps_z((s + LA - 2) // 2)
+            if XX_PRO + s < 16:
+                square_x_emb((XX_PRO + s) // 2, (XX_PRO + s) % 2)
+            if s + LA == 15:
+                root_z(7)
+                add_eps_z(7)
+            if s == RX_AT + 2:
+                keep_rx_row(0)
+                keep_rx_row(1)
+            if s == RX_AT:
+                nc.gpsimd.tensor_copy(out=beta_f[:], in_=beta_bf[:])
+                x_norms()
+            if s == RX_AT + 1:
+                nc.vector.reciprocal(out=rx[:], in_=x_norm_eps[:])
+            for k in LOGS.get(s, []):
+                logarithm(k)
+            for k in POWERS.get(s, []):
+                power_and_store(k)
+        for part in range(2):
+            for h in range(4):
+                multiply_half(15, h, part)
+                if h == 0 and part == 0:
+                    turn(13)
+                    turn(14)
+                    first_term(14, nc.gpsimd)
+                take_head(15, h, False, part)
+                if part == 0 and h == 1:
+                    add_second_term(13)
+                if part == 0 and h == 2:
+                    logarithm(12)
+                    logarithm(13)
+                    add_second_term(14)
+                if part == 0 and h == 3:
+                    logarithm(14)
+                if part == 1 and h == 0:
+                    first_term(15, nc.vector, 0, 2)
+                    turn(15, 0, 2)
+                if part == 1 and h == 1:
+                    add_second_term(15, 0, 2)
+        first_term(15, nc.vector, 2, 4)
+        turn(15, 2, 4)
+        logarithm(15, 0, 2)
+        add_second_term(15, 2, 4)
+        logarithm(15, 2, 4)
+        for k in with_mirror:
+            if k < 12:
+                mirror(k, "vector")
+        for k in (12, 13, 14):
+            power_and_store(k)
+        power_and_store(15, 0, 2)
+        power_and_store(15, 2, 4)
+        for k in (12, 13, 14):
+            mirror(k, "vector")
+        mirror(15, "vector", 0, 2)
+        mirror(15, "vector", 2, 4)

@@ -19,7 +19,7 @@ Z_BUFFERS = 7
 RX_AT = 7
 LA = 4
 EARLY = 7
-ZC_A = {10, 11}
+ZC_A = {9, 10, 11}
 ZC_B = set(range(12))
 OWN = {10: [0, 2, 4, 6, 8, 9], 11: [10], 12: [11], 13: [12], 14: [13]}
 FINISH = {10: [0, 2], 11: [4, 6], 12: [8, 9, 10], 13: [11], 14: [12], 15: []}
@@ -28,7 +28,7 @@ LOGS = {12: [0, 2, 4, 6], 13: [8, 9, 10, 11]}
 POWERS = {14: [0, 2, 4, 6, 8, 9, 10, 11]}
 X_ON_S = {2, 3, 7}
 XE_ON_S = {(2, 0), (3, 0), (2, 1), (3, 1)}
-H0_ON_V = set(range(16))
+H0_ON_V = set(range(12)) | {14, 15}
 XX_FIRST = 6
 XX_PRO = 9
 FIRST_BATCH = 12
@@ -439,42 +439,58 @@ def tile_affnet_t_kernel(tc, X, W, Z, beta, out):
             add_eps_z(1)
 
         transpose_z(4)
+        multiply(0, 0)
+        take_head(0, 0, 0 not in H0_ON_V)
         for s in range(15):
-            for h in range(4):
+            for h in range(1, 4):
                 multiply(s, h)
+            if s < 14:
+                multiply(s + 1, 0)
+            else:
+                multiply_half(15, 0, 0)
             if s + 5 < 16:
                 transpose_z(s + 5)
-            between = [[], [], [], [], []]
-            if s + 4 < 16:
-                i, heads = half_row(s + 4)
-                between[1].append(lambda i=i, h=heads[0]: copy_z(i, h, "scalar" if s in ZC_A else "vector"))
-                between[2].append(lambda i=i, h=heads[1]: copy_z(i, h, "scalar" if s in ZC_B else "vector"))
-            for n, k in enumerate(FINISH.get(s, [])):
-                between[FSLOT[s][n]].append(lambda k=k: add_second_term(k))
-            if s % 2 == 0 and s + 3 < 16:
-                between[3].append(lambda s=s: quantise_z((s + 3) // 2))
+            odd = s % 2
+            i_root = (s + LA - 2) // 2
+            has_root = s % 2 == LA % 2 and 2 <= i_root < 7
             for k in OWN.get(s, []):
                 first_term(k, nc.gpsimd)
-            for h in range(4):
-                take_head(s, h, first_on_scalar=s not in H0_ON_V)
-                if h == 0 and s % 2 == LA % 2 and (2 if LA > 3 else 1) <= (s + LA - 2) // 2 < EARLY:
-                    root_z((s + LA - 2) // 2)
-                if h == (0 if LA > 3 else 3) and s % 2 == 1 and s // 2 + 1 < 8:
-                    invert_z(s // 2 + 1)
-                if h == (3 if s < 12 else 0):
-                    for k in FINISH.get(s, []):
-                        turn(k)
-                for piece in between[h]:
-                    piece()
-            for piece in between[4]:
-                piece()
+            if odd and s // 2 + 1 < 8:
+                invert_z(s // 2 + 1)
+            if has_root:
+                root_z(i_root)
+            take_head(s, 1, False)
+            if s + 4 < 16:
+                i, heads = half_row(s + 4)
+                copy_z(i, heads[0], "scalar" if s in ZC_A else "vector")
+                copy_z(i, heads[1], "scalar" if s in ZC_B else "vector")
+            finish = list(FINISH.get(s, []))
+            for k in finish:
+                turn(k)
+            def next_product():
+                if s < 14:
+                    take_head(s + 1, 0, s + 1 not in H0_ON_V)
+                else:
+                    take_head(15, 0, False, 0)
+            if s > 11:
+                next_product()
+            take_head(s, 2, False)
+            if s < 12:
+                next_product()
+            elif finish:
+                add_second_term(finish.pop(0))
+            take_head(s, 3, False)
+            for k in finish:
+                add_second_term(k)
+            if not odd and s + 3 < 16:
+                quantise_z((s + 3) // 2)
             if s == RX_AT + 2:
                 spread_rx(0)
                 spread_rx(1)
             if s + LA < 16:
                 square_z(s + LA)
-            if s % 2 == LA % 2 and (2 if LA > 3 else 1) <= (s + LA - 2) // 2 < EARLY:
-                add_eps_z((s + LA - 2) // 2)
+            if has_root:
+                add_eps_z(i_root)
             if XX_PRO + s < 16:
                 square_x_emb((XX_PRO + s) // 2, (XX_PRO + s) % 2)
             if s + LA == 15:
@@ -492,34 +508,39 @@ def tile_affnet_t_kernel(tc, X, W, Z, beta, out):
                 logarithm(k)
             for k in POWERS.get(s, []):
                 power_and_store(k)
-        for part in range(2):
-            for h in range(4):
-                multiply_half(15, h, part)
-                if h == 0 and part == 0:
-                    turn(13)
-                    turn(14)
-                    first_term(14, nc.gpsimd)
-                take_head(15, h, False, part)
-                if part == 0 and h == 1:
-                    add_second_term(13)
-                if part == 0 and h == 2:
-                    logarithm(12)
-                    logarithm(13)
-                    add_second_term(14)
-                if part == 0 and h == 3:
-                    logarithm(14)
-                if part == 1 and h == 0:
-                    first_term(15, nc.vector, 0, 2)
-                    turn(15, 0, 2)
-                if part == 1 and h == 1:
-                    add_second_term(15, 0, 2)
+        for h in range(1, 4):
+            multiply_half(15, h, 0)
+        multiply_half(15, 0, 1)
+        first_term(14, nc.gpsimd)
+        turn(13)
+        turn(14)
+        take_head(15, 1, False, 0)
+        add_second_term(13)
+        take_head(15, 2, False, 0)
+        take_head(15, 0, False, 1)
+        multiply_half(15, 1, 1)
+        multiply_half(15, 2, 1)
+        take_head(15, 3, False, 0)
+        multiply_half(15, 3, 1)
+        add_second_term(14)
+        turn(15, 0, 2)
+        take_head(15, 1, False, 1)
+        first_term(15, nc.vector, 0, 2)
+        take_head(15, 2, False, 1)
+        add_second_term(15, 0, 2)
+        take_head(15, 3, False, 1)
+        logarithm(12)
+        logarithm(13)
+        logarithm(14)
+        logarithm(15, 0, 2)
+        mirror(2, "vector")
         first_term(15, nc.vector, 2, 4)
         turn(15, 2, 4)
-        logarithm(15, 0, 2)
+        mirror(4, "vector")
         add_second_term(15, 2, 4)
         logarithm(15, 2, 4)
         for k in with_mirror:
-            if k < 12:
+            if 4 < k < 12:
                 mirror(k, "vector")
         for k in (12, 13, 14):
             power_and_store(k)

@@ -21,7 +21,7 @@ LA = 4
 EARLY = 7
 ZC_A = {9, 10, 11}
 ZC_B = set(range(12))
-OWN = {10: [0, 2, 4, 6, 8, 9], 11: [10], 12: [11], 13: [12], 14: [13]}
+OWN = {10: [0, 2, 4, 6, 8], 11: [9, 10], 12: [11], 13: [12], 14: [13]}
 FINISH = {10: [0, 2], 11: [4, 6], 12: [8, 9, 10], 13: [11], 14: [12], 15: []}
 FSLOT = {10: [3, 4], 11: [3, 4], 12: [1, 2, 4], 13: [2], 14: [2], 15: []}
 LOGS = {12: [0, 2, 4, 6], 13: [8, 9, 10, 11]}
@@ -29,7 +29,7 @@ POWERS = {14: [0, 2, 4, 6, 8, 9, 10, 11]}
 X_ON_S = {2, 3, 7}
 XE_ON_S = {(2, 0), (3, 0), (2, 1), (3, 1)}
 H0_ON_V = set(range(12)) | {14, 15}
-XX_FIRST = 6
+XX_FIRST = 4
 XX_PRO = 9
 FIRST_BATCH = 12
 
@@ -372,18 +372,17 @@ def tile_affnet_t_kernel(tc, X, W, Z, beta, out):
         load_x_tile(3)
         for a in range(4):
             load_w_piece(a, 1)
-        load_z(0)
         load_x_second_half()
-        for i in range(1, Z_BUFFERS):
+        for i in range(Z_BUFFERS):
             load_z(i)
 
         turn_x(0)
         turn_x(1)
         copy_x(0)
         copy_x(1)
-        quantise_x(0, 2)
         regroup_w("vector", 0, 0)
         regroup_w("scalar", 0, 1)
+        quantise_x(0, 2)
         regroup_w("vector", 1, 0)
         regroup_w("scalar", 1, 1)
         turn_x(2)
@@ -397,46 +396,46 @@ def tile_affnet_t_kernel(tc, X, W, Z, beta, out):
         regroup_w("scalar", 0, 3)
         for m in range(2):
             x_emb_transposed(m, 0)
-        regroup_w("vector", 1, 2)
+        regroup_w("gpsimd", 1, 2)
         regroup_w("scalar", 1, 3)
         for m in range(2, 4):
             x_emb_transposed(m, 0)
+        for m in range(4, 8):
+            turn_x(m)
         quantise_w(0, 1)
         quantise_w(1, 1)
+        for m in range(4, 8):
+            copy_x(m)
         square_head(0, 0)
         for m in range(4):
             x_emb_transposed(m, 1)
         square_head(0, 1)
-        for m in range(4, 8):
-            turn_x(m)
-            copy_x(m)
-        transpose_and_copy_z(0)
         quantise_x(4, 4)
-        quantise_x_emb(0)
+        transpose_and_copy_z(0)
         for u in range(XX_FIRST):
             square_x_emb(u // 2, u % 2)
-        transpose_and_copy_z(1)
+        quantise_x_emb(0)
         for m in range(4, 8):
             x_emb_transposed(m, 0)
         square_head(0, 2)
         square_head(0, 3)
+        root_z(0)
+        add_eps_z(0)
+        transpose_and_copy_z(1)
         for m in range(4, 8):
             x_emb_transposed(m, 1)
         load_z(7)
-        root_z(0)
+        square_z(2)
         for u in range(XX_FIRST, XX_PRO):
             square_x_emb(u // 2, u % 2)
-        add_eps_z(0)
         quantise_z(0)
         transpose_and_copy_z(2)
         invert_z(0)
         quantise_x_emb(1)
         transpose_and_copy_z(3)
-        for z in range(2, LA):
-            square_z(z)
-        if LA > 3:
-            root_z(1)
-            add_eps_z(1)
+        square_z(3)
+        root_z(1)
+        add_eps_z(1)
 
         transpose_z(4)
         multiply(0, 0)
@@ -467,6 +466,9 @@ def tile_affnet_t_kernel(tc, X, W, Z, beta, out):
             finish = list(FINISH.get(s, []))
             for k in finish:
                 turn(k)
+            if s == 14:
+                turn(13)
+                turn(14)
             def next_product():
                 if s < 14:
                     take_head(s + 1, 0, s + 1 not in H0_ON_V)
@@ -484,9 +486,8 @@ def tile_affnet_t_kernel(tc, X, W, Z, beta, out):
                 add_second_term(k)
             if not odd and s + 3 < 16:
                 quantise_z((s + 3) // 2)
-            if s == RX_AT + 2:
-                spread_rx(0)
-                spread_rx(1)
+            if s in (RX_AT + 2, RX_AT + 3):
+                spread_rx(s - RX_AT - 2)
             if s + LA < 16:
                 square_z(s + LA)
             if has_root:
@@ -496,9 +497,8 @@ def tile_affnet_t_kernel(tc, X, W, Z, beta, out):
             if s + LA == 15:
                 root_z(7)
                 add_eps_z(7)
-            if s == RX_AT + 2:
-                keep_rx_row(0)
-                keep_rx_row(1)
+            if s in (RX_AT + 2, RX_AT + 3):
+                keep_rx_row(s - RX_AT - 2)
             if s == RX_AT:
                 nc.gpsimd.tensor_copy(out=beta_f[:], in_=beta_bf[:])
                 x_norms()
@@ -512,8 +512,6 @@ def tile_affnet_t_kernel(tc, X, W, Z, beta, out):
             multiply_half(15, h, 0)
         multiply_half(15, 0, 1)
         first_term(14, nc.gpsimd)
-        turn(13)
-        turn(14)
         take_head(15, 1, False, 0)
         add_second_term(13)
         take_head(15, 2, False, 0)

@@ -18,17 +18,18 @@ BANKS = 4
 Z_BUFFERS = 7
 RX_AT = 7
 LA = 4
+CL = 3
 EARLY = 7
-ZC_A = {9, 10, 11}
-ZC_B = set(range(12))
+ZC_A = {9, 11}
+ZC_B = set(range(13))
 OWN = {10: [0, 2, 4, 6, 8], 11: [9, 10], 12: [11], 13: [12], 14: [13]}
-FINISH = {10: [0, 2], 11: [4, 6], 12: [8, 9, 10], 13: [11], 14: [12], 15: []}
+FINISH = {10: [0, 2], 11: [4, 6], 12: [8, 9, 10], 13: [11], 14: [12]}
 FSLOT = {10: [3, 4], 11: [3, 4], 12: [1, 2, 4], 13: [2], 14: [2], 15: []}
-LOGS = {12: [0, 2, 4, 6], 13: [8, 9, 10, 11]}
-POWERS = {14: [0, 2, 4, 6, 8, 9, 10, 11]}
+LOGS = {12: [(0, 6)], 13: [(8, 9), (10, 11)]}
+POWERS = {14: [(0, 6), (8, 9), (10, 11)]}
 X_ON_S = {2, 3, 7}
 XE_ON_S = {(2, 0), (3, 0), (2, 1), (3, 1)}
-H0_ON_V = set(range(12)) | {14, 15}
+H0_ON_V = set(range(13)) | {14, 15}
 XX_FIRST = 4
 XX_PRO = 9
 FIRST_BATCH = 12
@@ -309,12 +310,21 @@ def tile_affnet_t_kernel(tc, X, W, Z, beta, out):
         with_blocks = [s for s in range(16) if blocks_of(s)[1] > 0]
         with_mirror = [s for s in range(16) if min(blocks_of(s)[1], s // 2 - blocks_of(s)[0]) > 0]
 
+        places = {}
+        for n, group in enumerate(((0, 2, 4, 6, 8, 9), (10, 11, 12, 13), (14, 15))):
+            start = 0
+            for s in group:
+                places[s] = (n, start)
+                start += blocks_of(s)[1] * P
+
+        def results(first, last, lo=0, hi=4):
+            n, start = places[first]
+            if ("result", n) not in late:
+                late[("result", n)] = group_pool.tile([P, 2048], F32, name="results", tag="groups", align_bytes=64)
+            return late[("result", n)][:, start + lo * P:places[last][1] + min(hi, blocks_of(last)[1]) * P]
+
         def result(s):
-            n = with_blocks.index(s)
-            if ("result", n // 4) not in late:
-                late[("result", n // 4)] = group_pool.tile([P, 4, 512], F32, name="results", tag="groups",
-                                                           align_bytes=64)
-            return late[("result", n // 4)][:, n % 4, :]
+            return results(s, s)
 
         def first_term(s, engine, lo=0, hi=4):
             first, count = blocks_of(s)
@@ -322,10 +332,10 @@ def tile_affnet_t_kernel(tc, X, W, Z, beta, out):
             cols = slice(P * first + part.start, P * first + part.stop)
             engine.tensor_tensor(out=result(s)[:, part], in0=b[j][:, cols], in1=rx_row[:, cols], op=ALU.mult)
 
-        def turn(s, lo=0, hi=4):
+        def turn(s, kind="tr", lo=0, hi=4):
             first, count = blocks_of(s)
             j = s // 2
-            banks[("turned", s, lo)] = bank("tr", [P, 4, P])
+            banks[("turned", s, lo)] = bank(kind, [P, 4, P])
             for k in range(lo, min(hi, count)):
                 nc.tensor.transpose(banks[("turned", s, lo)][:, k, :], b[first + k][:, j * P:(j + 1) * P], ident[:])
 
@@ -337,14 +347,17 @@ def tile_affnet_t_kernel(tc, X, W, Z, beta, out):
                                            scalar=rx[:, j:j + 1], in1=result(s)[:, part],
                                            op0=ALU.mult, op1=ALU.add)
 
-        def logarithm(s, lo=0, hi=4):
-            part = slice(lo * P, min(hi, blocks_of(s)[1]) * P)
-            nc.scalar.activation(out=result(s)[:, part], in_=result(s)[:, part], func=ACT.Ln, bias=0.5, scale=0.25)
+        def logarithm(s, last=None, lo=0, hi=4):
+            part = results(s, s if last is None else last, lo, hi)
+            nc.scalar.activation(out=part, in_=part, func=ACT.Ln, bias=0.5, scale=0.25)
 
-        def power_and_store(s, lo=0, hi=4):
+        def power(s, last=None, lo=0, hi=4):
+            part = results(s, s if last is None else last, lo, hi)
+            nc.scalar.activation(out=part, in_=part, func=ACT.Exp, scale=beta_f[:, 0:1])
+
+        def store(s, lo=0, hi=4):
             first, count = blocks_of(s)
             j, part = s // 2, slice(lo * P, min(hi, count) * P)
-            nc.scalar.activation(out=result(s)[:, part], in_=result(s)[:, part], func=ACT.Exp, scale=beta_f[:, 0:1])
             nc.sync.dma_start(out=out[j * P:(j + 1) * P, P * first + part.start:P * first + part.stop],
                               in_=result(s)[:, part])
 
@@ -426,29 +439,38 @@ def tile_affnet_t_kernel(tc, X, W, Z, beta, out):
             x_emb_transposed(m, 1)
         load_z(7)
         square_z(2)
+        transpose_z(2)
         for u in range(XX_FIRST, XX_PRO):
             square_x_emb(u // 2, u % 2)
         quantise_z(0)
-        transpose_and_copy_z(2)
+        copy_z(1, 0)
+        copy_z(1, 1)
         invert_z(0)
         quantise_x_emb(1)
-        transpose_and_copy_z(3)
+        if CL > 3:
+            transpose_and_copy_z(3)
         square_z(3)
         root_z(1)
         add_eps_z(1)
 
-        transpose_z(4)
+        transpose_z(CL)
         multiply(0, 0)
         take_head(0, 0, 0 not in H0_ON_V)
         for s in range(15):
-            for h in range(1, 4):
-                multiply(s, h)
+            finish = list(FINISH.get(s, []))
+            early = s + CL + 1 < 15
+            multiply(s, 1)
+            if s > 12:
+                for k in finish:
+                    turn(k)
+            multiply(s, 2)
+            multiply(s, 3)
             if s < 14:
                 multiply(s + 1, 0)
             else:
                 multiply_half(15, 0, 0)
-            if s + 5 < 16:
-                transpose_z(s + 5)
+            if s + CL + 1 < 16:
+                transpose_z(s + CL + 1)
             odd = s % 2
             i_root = (s + LA - 2) // 2
             has_root = s % 2 == LA % 2 and 2 <= i_root < 7
@@ -459,13 +481,15 @@ def tile_affnet_t_kernel(tc, X, W, Z, beta, out):
             if has_root:
                 root_z(i_root)
             take_head(s, 1, False)
-            if s + 4 < 16:
-                i, heads = half_row(s + 4)
+            if s + CL < 16:
+                i, heads = half_row(s + CL)
                 copy_z(i, heads[0], "scalar" if s in ZC_A else "vector")
                 copy_z(i, heads[1], "scalar" if s in ZC_B else "vector")
-            finish = list(FINISH.get(s, []))
-            for k in finish:
-                turn(k)
+            if not early and s < 13:
+                for k in finish:
+                    turn(k)
+            if s > 12:
+                add_second_term(finish.pop(0))
             if s == 14:
                 turn(13)
                 turn(14)
@@ -474,17 +498,17 @@ def tile_affnet_t_kernel(tc, X, W, Z, beta, out):
                     take_head(s + 1, 0, s + 1 not in H0_ON_V)
                 else:
                     take_head(15, 0, False, 0)
-            if s > 11:
-                next_product()
             take_head(s, 2, False)
-            if s < 12:
-                next_product()
-            elif finish:
-                add_second_term(finish.pop(0))
+            next_product()
             take_head(s, 3, False)
+            if early:
+                for k in finish:
+                    turn(k, "mx")
+            if not odd and s + 3 < 16 and early:
+                quantise_z((s + 3) // 2)
             for k in finish:
                 add_second_term(k)
-            if not odd and s + 3 < 16:
+            if not odd and not early and s + 3 < 16:
                 quantise_z((s + 3) // 2)
             if s in (RX_AT + 2, RX_AT + 3):
                 spread_rx(s - RX_AT - 2)
@@ -504,10 +528,13 @@ def tile_affnet_t_kernel(tc, X, W, Z, beta, out):
                 x_norms()
             if s == RX_AT + 1:
                 nc.vector.reciprocal(out=rx[:], in_=x_norm_eps[:])
-            for k in LOGS.get(s, []):
-                logarithm(k)
-            for k in POWERS.get(s, []):
-                power_and_store(k)
+            for k, last in LOGS.get(s, []):
+                logarithm(k, last)
+            for k, last in POWERS.get(s, []):
+                power(k, last)
+                for n in with_blocks:
+                    if k <= n <= last:
+                        store(n)
         for h in range(1, 4):
             multiply_half(15, h, 0)
         multiply_half(15, 0, 1)
@@ -521,29 +548,30 @@ def tile_affnet_t_kernel(tc, X, W, Z, beta, out):
         take_head(15, 3, False, 0)
         multiply_half(15, 3, 1)
         add_second_term(14)
-        turn(15, 0, 2)
+        turn(15, "tr", 0, 2)
         take_head(15, 1, False, 1)
         first_term(15, nc.vector, 0, 2)
         take_head(15, 2, False, 1)
         add_second_term(15, 0, 2)
         take_head(15, 3, False, 1)
-        logarithm(12)
-        logarithm(13)
+        logarithm(12, 13)
         logarithm(14)
-        logarithm(15, 0, 2)
+        logarithm(15, 15, 0, 2)
         mirror(2, "vector")
         first_term(15, nc.vector, 2, 4)
-        turn(15, 2, 4)
+        turn(15, "tr", 2, 4)
         mirror(4, "vector")
         add_second_term(15, 2, 4)
-        logarithm(15, 2, 4)
+        logarithm(15, 15, 2, 4)
         for k in with_mirror:
             if 4 < k < 12:
                 mirror(k, "vector")
         for k in (12, 13, 14):
-            power_and_store(k)
-        power_and_store(15, 0, 2)
-        power_and_store(15, 2, 4)
+            power(k)
+            store(k)
+        for part in range(2):
+            power(15, 15, 2 * part, 2 * part + 2)
+            store(15, 2 * part, 2 * part + 2)
         for k in (12, 13, 14):
             mirror(k, "vector")
         mirror(15, "vector", 0, 2)

@@ -20,16 +20,16 @@ RX_AT = 7
 LA = 4
 CL = 3
 EARLY = 7
-ZC_A = {9, 11}
+ZC_A = {9, 10, 11, 12}
 ZC_B = set(range(13))
-OWN = {10: [0, 2, 4, 6, 8], 11: [9, 10], 12: [11], 13: [12], 14: [13]}
+OWN = {9: [0, 2, 4, 6], 10: [8], 11: [9, 10], 12: [11], 13: [12], 14: [13]}
 FINISH = {10: [0, 2], 11: [4, 6], 12: [8, 9, 10], 13: [11], 14: [12]}
 FSLOT = {10: [3, 4], 11: [3, 4], 12: [1, 2, 4], 13: [2], 14: [2], 15: []}
 LOGS = {12: [(0, 6)], 13: [(8, 9), (10, 11)]}
 POWERS = {14: [(0, 6), (8, 9), (10, 11)]}
 X_ON_S = {2, 3, 7}
 XE_ON_S = {(2, 0), (3, 0), (2, 1), (3, 1)}
-H0_ON_V = set(range(13)) | {14, 15}
+H0_ON_V = set(range(16)) - {13}
 XX_FIRST = 4
 XX_PRO = 9
 FIRST_BATCH = 12
@@ -67,10 +67,12 @@ def tile_affnet_t_kernel(tc, X, W, Z, beta, out):
 
         ident = const.tile([P, P], F32)
         make_identity(nc, ident[:])
-        half = const.tile([P, 1], F32)
+        half = const.tile([P, 8], F32)
         nc.vector.memset(half[:], 0.5)
+        minus_one = const.tile([P, 8], F32)
+        nc.vector.memset(minus_one[:], -1.0)
         warm = const.tile([P, 1], F32)
-        nc.scalar.activation(out=warm[:], in_=half[:, 0:1], func=ACT.Sqrt)
+        nc.scalar.activation(out=warm[:], in_=half[:, 0:1], func=ACT.Ln)
         beta_bf = const.tile([P, 1], BF16)
         nc.scalar.dma_start(out=beta_bf[:], in_=beta.partition_broadcast(P))
         beta_f = const.tile([P, 1], F32)
@@ -169,17 +171,14 @@ def tile_affnet_t_kernel(tc, X, W, Z, beta, out):
             for h in heads:
                 square_head(i, h)
 
-        def root_z(i):
-            c = slice(4 * i, 4 * i + 4)
-            nc.scalar.activation(out=z_norm[:, c], in_=z_sq[:, c], func=ACT.Sqrt)
+        def norms(squares, norm, norm_eps, inverse, count):
+            nc.gpsimd.tensor_tensor(out=norm, in0=squares, in1=half[:, 0:count], op=ALU.pow)
+            nc.gpsimd.tensor_scalar(out=norm_eps, in0=norm, scalar1=EPS, scalar2=1.0, op0=ALU.add, op1=ALU.mult)
+            nc.gpsimd.tensor_tensor(out=inverse, in0=norm_eps, in1=minus_one[:, 0:count], op=ALU.pow)
 
-        def add_eps_z(i):
+        def norms_z(i):
             c = slice(4 * i, 4 * i + 4)
-            nc.scalar.activation(out=z_norm_eps[:, c], in_=z_norm[:, c], func=ACT.Copy, bias=EPS)
-
-        def invert_z(i):
-            c = slice(4 * i, 4 * i + 4)
-            nc.vector.reciprocal(out=rz[:, c], in_=z_norm_eps[:, c])
+            norms(z_sq[:, c], z_norm[:, c], z_norm_eps[:, c], rz[:, c], 4)
 
         def turn_x(m):
             transpose_words(("x", m), x_rows[:, m, :])
@@ -242,8 +241,7 @@ def tile_affnet_t_kernel(tc, X, W, Z, beta, out):
         def x_norms():
             pairs = x_sq_halves[:].rearrange("p (m c) -> p m c", c=2)
             nc.gpsimd.tensor_tensor(out=x_sq[:], in0=pairs[:, :, 0], in1=pairs[:, :, 1], op=ALU.add)
-            nc.scalar.activation(out=x_norm[:], in_=x_sq[:], func=ACT.Sqrt)
-            nc.scalar.activation(out=x_norm_eps[:], in_=x_norm[:], func=ACT.Copy, bias=EPS)
+            norms(x_sq[:], x_norm[:], x_norm_eps[:], rx[:], 8)
 
         def spread_rx(c):
             banks[("row", c)] = bank("mx", [P, 512])
@@ -432,8 +430,7 @@ def tile_affnet_t_kernel(tc, X, W, Z, beta, out):
             x_emb_transposed(m, 0)
         square_head(0, 2)
         square_head(0, 3)
-        root_z(0)
-        add_eps_z(0)
+        norms_z(0)
         transpose_and_copy_z(1)
         for m in range(4, 8):
             x_emb_transposed(m, 1)
@@ -445,13 +442,11 @@ def tile_affnet_t_kernel(tc, X, W, Z, beta, out):
         quantise_z(0)
         copy_z(1, 0)
         copy_z(1, 1)
-        invert_z(0)
         quantise_x_emb(1)
         if CL > 3:
             transpose_and_copy_z(3)
         square_z(3)
-        root_z(1)
-        add_eps_z(1)
+        norms_z(1)
 
         transpose_z(CL)
         multiply(0, 0)
@@ -472,14 +467,8 @@ def tile_affnet_t_kernel(tc, X, W, Z, beta, out):
             if s + CL + 1 < 16:
                 transpose_z(s + CL + 1)
             odd = s % 2
-            i_root = (s + LA - 2) // 2
-            has_root = s % 2 == LA % 2 and 2 <= i_root < 7
             for k in OWN.get(s, []):
                 first_term(k, nc.gpsimd)
-            if odd and s // 2 + 1 < 8:
-                invert_z(s // 2 + 1)
-            if has_root:
-                root_z(i_root)
             take_head(s, 1, False)
             if s + CL < 16:
                 i, heads = half_row(s + CL)
@@ -510,24 +499,19 @@ def tile_affnet_t_kernel(tc, X, W, Z, beta, out):
                 add_second_term(k)
             if not odd and not early and s + 3 < 16:
                 quantise_z((s + 3) // 2)
-            if s in (RX_AT + 2, RX_AT + 3):
-                spread_rx(s - RX_AT - 2)
+            if s in (RX_AT + 1, RX_AT + 2):
+                spread_rx(s - RX_AT - 1)
             if s + LA < 16:
                 square_z(s + LA)
-            if has_root:
-                add_eps_z(i_root)
+                if (s + LA) % 2 == 1:
+                    norms_z((s + LA) // 2)
             if XX_PRO + s < 16:
                 square_x_emb((XX_PRO + s) // 2, (XX_PRO + s) % 2)
-            if s + LA == 15:
-                root_z(7)
-                add_eps_z(7)
-            if s in (RX_AT + 2, RX_AT + 3):
-                keep_rx_row(s - RX_AT - 2)
-            if s == RX_AT:
+            if s in (RX_AT + 1, RX_AT + 2):
+                keep_rx_row(s - RX_AT - 1)
+            if s == RX_AT - 1:
                 nc.gpsimd.tensor_copy(out=beta_f[:], in_=beta_bf[:])
                 x_norms()
-            if s == RX_AT + 1:
-                nc.vector.reciprocal(out=rx[:], in_=x_norm_eps[:])
             for k, last in LOGS.get(s, []):
                 logarithm(k, last)
             for k, last in POWERS.get(s, []):

from contextlib import ExitStack

import concourse.mybir as mybir
from concourse.masks import make_identity

FLOPS = 2 * 1024 * 1024 * 1024 * 5

BF16 = mybir.dt.bfloat16
F32 = mybir.dt.float32
U32 = mybir.dt.uint32
U8 = mybir.dt.uint8
FP8X4 = mybir.dt.float8_e4m3fn_x4
ACT = mybir.ActivationFunctionType
ALU = mybir.AluOpType
P = 128
EPS = 1e-6
BANKS = 4
Z_BUFFERS = 7
RX_AT = 7
LA = 4
CL = 3
EARLY = 7
ZC_A = {9, 10, 11, 12}
ZC_B = set(range(13))
OWN = {9: [0, 2, 4, 6], 10: [8], 11: [9, 10], 12: [11], 13: [12], 14: [13]}
FINISH = {10: [0, 2], 11: [4, 6], 12: [8, 9, 10], 13: [11], 14: [12]}
FSLOT = {10: [3, 4], 11: [3, 4], 12: [1, 2, 4], 13: [2], 14: [2], 15: []}
LOGS = {12: [(0, 6)], 13: [(8, 9), (10, 11)]}
POWERS = {14: [(0, 6), (8, 9), (10, 11)]}
X_ON_S = {2, 3, 7}
XE_ON_S = {(2, 0), (3, 0), (2, 1), (3, 1)}
H0_ON_V = set(range(16)) - {13}
XX_FIRST = 4
XX_PRO = 9
FIRST_BATCH = 12


def blocks_of(s):
    first = 4 * (s % 2)
    return first, max(0, min(s // 2, first + 3) - first + 1)


def tile_affnet_t_kernel(tc, X, W, Z, beta, out):
    nc = tc.nc
    with ExitStack() as ctx:
        const = ctx.enter_context(tc.tile_pool(name="const", bufs=1))
        keep = ctx.enter_context(tc.tile_pool(name="keep", bufs=1))
        z_pool = ctx.enter_context(tc.tile_pool(name="z_pool", bufs=Z_BUFFERS))
        zg_pool = ctx.enter_context(tc.tile_pool(name="zg_pool", bufs=2))
        shared = ctx.enter_context(tc.tile_pool(name="shared", bufs=1))
        group_pool = ctx.enter_context(tc.tile_pool(name="group_pool", bufs=3))
        psum = ctx.enter_context(tc.psum_pool(name="psum", bufs=1))

        taken = {"mx": 0, "tr": 0}

        def bank(kind, shape):
            taken[kind] += 1
            return psum.tile(shape, F32, name="bank", tag="%s%d" % (kind, taken[kind] % BANKS))

        def copy(engine, dst, src):
            if engine == "vector":
                nc.vector.tensor_copy(out=dst, in_=src)
            elif engine == "scalar":
                nc.scalar.copy(out=dst, in_=src)
            else:
                nc.gpsimd.tensor_scalar(out=dst, in0=src, scalar1=1.0, scalar2=0.0, op0=ALU.mult, op1=ALU.add)

        ident = const.tile([P, P], F32)
        make_identity(nc, ident[:])
        half = const.tile([P, 8], F32)
        nc.vector.memset(half[:], 0.5)
        minus_one = const.tile([P, 8], F32)
        nc.vector.memset(minus_one[:], -1.0)
        warm = const.tile([P, 1], F32)
        nc.scalar.activation(out=warm[:], in_=half[:, 0:1], func=ACT.Ln)
        beta_bf = const.tile([P, 1], BF16)
        nc.scalar.dma_start(out=beta_bf[:], in_=beta.partition_broadcast(P))
        beta_f = const.tile([P, 1], F32)
        unwanted = const.tile([P, 4, 1024], BF16)
        squares_made = [0]

        def scratch():
            squares_made[0] += 1
            return unwanted[:, squares_made[0] % 4, :]

        ctx.enter_context(tc.manual_schedule())

        z_words = keep.tile([P, 8, 1024], U32, align_bytes=64)
        z_scales = keep.tile([P, 8, 1024], U8, align_bytes=64)
        xe_words = keep.tile([P, 2, 1024], U32, align_bytes=64)
        xe_scales = keep.tile([P, 2, 1024], U8, align_bytes=64)
        z_sq = keep.tile([P, 32], F32)
        z_norm = keep.tile([P, 32], F32)
        z_norm_eps = keep.tile([P, 32], F32)
        rz = keep.tile([P, 32], F32)
        x_sq_halves = keep.tile([P, 16], F32)
        x_sq = keep.tile([P, 8], F32)
        x_norm = keep.tile([P, 8], F32)
        x_norm_eps = keep.tile([P, 8], F32)
        rx = keep.tile([P, 8], F32)
        rx_row = keep.tile([P, 1024], F32)
        x_rows = shared.tile([P, 8, 1024], BF16, name="x_rows", tag="slot_a")
        w_rows = shared.tile([P, 2, 2, 4, 512], BF16, name="w_rows", tag="slot_b")
        x_words = shared.tile([P, 8, 256], U32, align_bytes=64)
        x_scales = shared.tile([P, 8, 256], U8, align_bytes=64)
        w_words = shared.tile([P, 2, 1024], U32, align_bytes=64)
        w_scales = shared.tile([P, 2, 1024], U8, align_bytes=64)
        xe_groups = shared.tile([P, 2, 1024, 4], BF16, name="xe_groups", tag="slot_c", align_bytes=64)

        z_rows = {}
        z_groups = {}
        x_groups = {}
        w_groups = {}
        banks = {}
        b = {}
        late = {}

        def load_x_tile(m):
            nc.sync.dma_start(out=x_rows[:, m, :], in_=X[m * P:(m + 1) * P, :])

        def load_x_second_half():
            nc.sync.dma_start(out=x_rows[:, 4:8, :], in_=X[512:1024, :].rearrange("(t p) f -> p t f", p=P))

        def load_w_piece(a, c):
            cols = slice(512 * c, 512 * (c + 1))
            nc.sync.dma_start(out=w_rows[:, c, a // 2, 2 * (a % 2):2 * (a % 2) + 2, :],
                              in_=W[256 * a:256 * (a + 1), cols].rearrange("(p e) c -> p e c", e=2))

        def load_z(i):
            z_rows[i] = z_pool.tile([P, 4, 1024], BF16, name="z_tile")
            nc.sync.dma_start(out=z_rows[i][:], in_=Z[:, i * P:(i + 1) * P, :].rearrange("h p k -> p h k"))

        def transpose_words(key, rows):
            words = rows.bitcast(F32)
            banks[key] = bank("tr", [P, 4, P])
            for a in range(4):
                nc.tensor.transpose(banks[key][:, a, :], words[:, a * P:(a + 1) * P], ident[:])

        def words_side_by_side(engine, dst, key):
            copy(engine, dst.bitcast(F32), banks[key][:].rearrange("p (g u) n -> p g n u", u=2))

        def half_row(z):
            return z // 2, (2 * (z % 2), 2 * (z % 2) + 1)

        def transpose_z(z):
            i, heads = half_row(z)
            for h in heads:
                transpose_words(("z", i, h), z_rows[i][:, h, :])

        def copy_z(i, h, engine="vector"):
            if i not in z_groups:
                z_groups[i] = zg_pool.tile([P, 4, 2, P, 4], BF16, name="z_group", align_bytes=64)
            words_side_by_side(engine, z_groups[i][:, h], ("z", i, h))

        def transpose_and_copy_z(z):
            i, heads = half_row(z)
            for h in heads:
                transpose_words(("z", i, h), z_rows[i][:, h, :])
                copy_z(i, h)

        def quantise_z(i):
            nc.vector.quantize_mx(out=z_words[:, i, :].bitcast(FP8X4), scales=z_scales[:, i, :],
                                  in_=z_groups[i][:].rearrange("p h g n t -> p (h g n t)"))

        def square_head(i, h):
            nc.scalar.activation(out=scratch(), in_=z_rows[i][:, h, :], func=ACT.Square,
                                 accum_out=z_sq[:, 4 * i + h:4 * i + h + 1])

        def square_z(z):
            i, heads = half_row(z)
            for h in heads:
                square_head(i, h)

        def norms(squares, norm, norm_eps, inverse, count):
            nc.gpsimd.tensor_tensor(out=norm, in0=squares, in1=half[:, 0:count], op=ALU.pow)
            nc.gpsimd.tensor_scalar(out=norm_eps, in0=norm, scalar1=EPS, scalar2=1.0, op0=ALU.add, op1=ALU.mult)
            nc.gpsimd.tensor_tensor(out=inverse, in0=norm_eps, in1=minus_one[:, 0:count], op=ALU.pow)

        def norms_z(i):
            c = slice(4 * i, 4 * i + 4)
            norms(z_sq[:, c], z_norm[:, c], z_norm_eps[:, c], rz[:, c], 4)

        def turn_x(m):
            transpose_words(("x", m), x_rows[:, m, :])

        def copy_x(m):
            if m // 4 not in x_groups:
                x_groups[m // 4] = group_pool.tile([P, 4, 2, P, 4], BF16, name="x_group", tag="groups", align_bytes=64)
            words_side_by_side("scalar" if m in X_ON_S else "vector", x_groups[m // 4][:, m % 4], ("x", m))

        def quantise_x(first_tile, count):
            tiles = slice(first_tile, first_tile + count)
            inner = slice(first_tile % 4, first_tile % 4 + count)
            nc.vector.quantize_mx(out=x_words[:, tiles, :].rearrange("p a b -> p (a b)").bitcast(FP8X4),
                                  scales=x_scales[:, tiles, :].rearrange("p a b -> p (a b)"),
                                  in_=x_groups[first_tile // 4][:, inner].rearrange("p j g n t -> p (j g n t)"))

        def regroup_w(engine, g, a):
            if g not in w_groups:
                w_groups[g] = group_pool.tile([P, 1024, 4], BF16, name="w_group", tag="groups", align_bytes=64)
            copy(engine, w_groups[g][:, 256 * a:256 * (a + 1), :].rearrange("p (f q) t -> p f q t", f=2),
                 w_rows[:, a // 2, g, :, 256 * (a % 2):256 * (a % 2 + 1)].rearrange("p t (q f) -> p f q t", f=2))

        def quantise_w(g, c):
            cols = slice(512 * c, 512 * (c + 1))
            nc.vector.quantize_mx(out=w_words[:, g, cols].bitcast(FP8X4), scales=w_scales[:, g, cols],
                                  in_=w_groups[g][:, cols, :].rearrange("p c t -> p (c t)"))

        def x_emb_transposed(m, big):
            acc = bank("mx", [P, 4, P])
            for t in range(4):
                col = (4 * big + t) * P
                for g in range(2):
                    nc.tensor.matmul_mx(out=acc[:, t, :],
                                        lhsT=w_words[:, g, col:col + P].bitcast(FP8X4),
                                        lhsT_scale=w_scales[:, g, col:col + P],
                                        rhs=x_words[:, m, g * P:(g + 1) * P].bitcast(FP8X4),
                                        rhs_scale=x_scales[:, m, g * P:(g + 1) * P],
                                        start=(g == 0), stop=(g == 1))
            copy("scalar" if (m, big) in XE_ON_S else "vector", xe_groups[:, big, m * P:(m + 1) * P, :],
                 acc[:].rearrange("p t m -> p m t"))

        def quantise_x_emb(c):
            cols = slice(512 * c, 512 * (c + 1))
            for big in range(2):
                nc.vector.quantize_mx(out=xe_words[:, big, cols].bitcast(FP8X4), scales=xe_scales[:, big, cols],
                                      in_=xe_groups[:, big, cols, :].rearrange("p m t -> p (m t)"))

        def square_x_emb(m, c):
            cols = slice(512 * c, 512 * (c + 1))
            acc = bank("mx", [P, 512])
            for g in range(2):
                nc.tensor.matmul_mx(out=acc[:],
                                    lhsT=x_words[:, m, g * P:(g + 1) * P].bitcast(FP8X4),
                                    lhsT_scale=x_scales[:, m, g * P:(g + 1) * P],
                                    rhs=w_words[:, g, cols].bitcast(FP8X4), rhs_scale=w_scales[:, g, cols],
                                    start=(g == 0), stop=(g == 1))
            nc.scalar.activation(out=scratch()[:, 0:512], in_=acc[:], func=ACT.Square,
                                 accum_out=x_sq_halves[:, 2 * m + c:2 * m + c + 1])

        def x_norms():
            pairs = x_sq_halves[:].rearrange("p (m c) -> p m c", c=2)
            nc.gpsimd.tensor_tensor(out=x_sq[:], in0=pairs[:, :, 0], in1=pairs[:, :, 1], op=ALU.add)
            norms(x_sq[:], x_norm[:], x_norm_eps[:], rx[:], 8)

        def spread_rx(c):
            banks[("row", c)] = bank("mx", [P, 512])
            for j in range(4):
                m = 4 * c + j
                nc.tensor.transpose(banks[("row", c)][:, j * P:(j + 1) * P], rx[:, m:m + 1].to_broadcast([P, P]), ident[:])

        def keep_rx_row(c):
            copy("scalar", rx_row[:, 512 * c:512 * (c + 1)], banks[("row", c)][:])

        def multiply(s, h):
            i, c = s // 2, s % 2
            cols = slice(512 * c, 512 * (c + 1))
            banks[("aff", s, h)] = bank("mx", [P, 512])
            for big in range(2):
                col = (2 * h + big) * P
                nc.tensor.matmul_mx(out=banks[("aff", s, h)][:],
                                    lhsT=z_words[:, i, col:col + P].bitcast(FP8X4),
                                    lhsT_scale=z_scales[:, i, col:col + P],
                                    rhs=xe_words[:, big, cols].bitcast(FP8X4), rhs_scale=xe_scales[:, big, cols],
                                    start=(big == 0), stop=(big == 1))

        def multiply_half(s, h, part):
            i, c = s // 2, s % 2
            cols = slice(512 * c + 256 * part, 512 * c + 256 * (part + 1))
            acc = bank("mx", [P, 256])
            for big in range(2):
                col = (2 * h + big) * P
                nc.tensor.matmul_mx(out=acc[:],
                                    lhsT=z_words[:, i, col:col + P].bitcast(FP8X4),
                                    lhsT_scale=z_scales[:, i, col:col + P],
                                    rhs=xe_words[:, big, cols].bitcast(FP8X4), rhs_scale=xe_scales[:, big, cols],
                                    start=(big == 0), stop=(big == 1))
            banks[("aff", s, h, part)] = acc

        def work(index):
            if "work" not in late:
                late["work"] = shared.tile([P, 8, 512], F32, name="work", tag="slot_c", align_bytes=64)
            return late["work"][:, index, :]

        def take_head(s, h, first_on_scalar, part=None):
            i, c = s // 2, s % 2
            acc = banks[("aff", s, h)] if part is None else banks[("aff", s, h, part)]
            scale = rz[:, 4 * i + h:4 * i + h + 1]
            base = 2 * (s % 2)
            some = slice(0, 512) if part is None else slice(256 * part, 256 * (part + 1))
            if h == 0:
                if first_on_scalar:
                    nc.scalar.activation(out=work(base)[:, some], in_=acc[:], func=ACT.Copy, scale=scale)
                else:
                    nc.vector.tensor_scalar_mul(out=work(base)[:, some], in0=acc[:], scalar1=scale)
                return
            if h == 3:
                if i not in b:
                    four_rows = shared.tile([P, 4, 1024], F32, name="four_rows", tag="slot_a" if i < 4 else "slot_b")
                    for k in range(4):
                        b[4 * (i // 4) + k] = four_rows[:, k, :]
                dst = b[i][:, 512 * c:512 * (c + 1)]
            else:
                dst = work(base + h % 2)
            nc.vector.scalar_tensor_tensor(out=dst[:, some], in0=acc[:], scalar=scale, in1=work(base + (h - 1) % 2)[:, some],
                                           op0=ALU.mult, op1=ALU.max)

        with_blocks = [s for s in range(16) if blocks_of(s)[1] > 0]
        with_mirror = [s for s in range(16) if min(blocks_of(s)[1], s // 2 - blocks_of(s)[0]) > 0]

        places = {}
        for n, group in enumerate(((0, 2, 4, 6, 8, 9), (10, 11, 12, 13), (14, 15))):
            start = 0
            for s in group:
                places[s] = (n, start)
                start += blocks_of(s)[1] * P

        def results(first, last, lo=0, hi=4):
            n, start = places[first]
            if ("result", n) not in late:
                late[("result", n)] = group_pool.tile([P, 2048], F32, name="results", tag="groups", align_bytes=64)
            return late[("result", n)][:, start + lo * P:places[last][1] + min(hi, blocks_of(last)[1]) * P]

        def result(s):
            return results(s, s)

        def first_term(s, engine, lo=0, hi=4):
            first, count = blocks_of(s)
            j, part = s // 2, slice(lo * P, min(hi, count) * P)
            cols = slice(P * first + part.start, P * first + part.stop)
            engine.tensor_tensor(out=result(s)[:, part], in0=b[j][:, cols], in1=rx_row[:, cols], op=ALU.mult)

        def turn(s, kind="tr", lo=0, hi=4):
            first, count = blocks_of(s)
            j = s // 2
            banks[("turned", s, lo)] = bank(kind, [P, 4, P])
            for k in range(lo, min(hi, count)):
                nc.tensor.transpose(banks[("turned", s, lo)][:, k, :], b[first + k][:, j * P:(j + 1) * P], ident[:])

        def add_second_term(s, lo=0, hi=4):
            first, count = blocks_of(s)
            j, part = s // 2, slice(lo * P, min(hi, count) * P)
            nc.vector.scalar_tensor_tensor(out=result(s)[:, part],
                                           in0=banks[("turned", s, lo)][:].rearrange("p a b -> p (a b)")[:, part],
                                           scalar=rx[:, j:j + 1], in1=result(s)[:, part],
                                           op0=ALU.mult, op1=ALU.add)

        def logarithm(s, last=None, lo=0, hi=4):
            part = results(s, s if last is None else last, lo, hi)
            nc.scalar.activation(out=part, in_=part, func=ACT.Ln, bias=0.5, scale=0.25)

        def power(s, last=None, lo=0, hi=4):
            part = results(s, s if last is None else last, lo, hi)
            nc.scalar.activation(out=part, in_=part, func=ACT.Exp, scale=beta_f[:, 0:1])

        def store(s, lo=0, hi=4):
            first, count = blocks_of(s)
            j, part = s // 2, slice(lo * P, min(hi, count) * P)
            nc.sync.dma_start(out=out[j * P:(j + 1) * P, P * first + part.start:P * first + part.stop],
                              in_=result(s)[:, part])

        def mirror(s, engine, lo=0, hi=4):
            first, count = blocks_of(s)
            j = s // 2
            hi = min(hi, count, j - first)
            turned = bank("tr", [P, 4, P])
            for k in range(lo, hi):
                nc.tensor.transpose(turned[:, k, :], result(s)[:, k * P:(k + 1) * P], ident[:])
            n = with_mirror.index(s)
            if ("mirror", n // 4) not in late:
                late[("mirror", n // 4)] = z_pool.tile([P, 4, 512], F32, name="z_tile")
            above = late[("mirror", n // 4)][:, n % 4, lo * P:hi * P]
            copy(engine, above, turned[:].rearrange("p a b -> p (a b)")[:, lo * P:hi * P])
            nc.sync.dma_start(
                out=out[(first + lo) * P:(first + hi) * P, j * P:(j + 1) * P].rearrange("(a i) c -> i a c", i=P),
                in_=above.rearrange("p (a c) -> p a c", c=P))

        load_x_tile(0)
        load_x_tile(1)
        for a in range(4):
            load_w_piece(a, 0)
        load_x_tile(2)
        load_x_tile(3)
        for a in range(4):
            load_w_piece(a, 1)
        load_x_second_half()
        for i in range(Z_BUFFERS):
            load_z(i)

        turn_x(0)
        turn_x(1)
        copy_x(0)
        copy_x(1)
        regroup_w("vector", 0, 0)
        regroup_w("scalar", 0, 1)
        quantise_x(0, 2)
        regroup_w("vector", 1, 0)
        regroup_w("scalar", 1, 1)
        turn_x(2)
        turn_x(3)
        quantise_w(0, 0)
        copy_x(2)
        quantise_w(1, 0)
        copy_x(3)
        quantise_x(2, 2)
        regroup_w("gpsimd", 0, 2)
        regroup_w("scalar", 0, 3)
        for m in range(2):
            x_emb_transposed(m, 0)
        regroup_w("gpsimd", 1, 2)
        regroup_w("scalar", 1, 3)
        for m in range(2, 4):
            x_emb_transposed(m, 0)
        for m in range(4, 8):
            turn_x(m)
        quantise_w(0, 1)
        quantise_w(1, 1)
        for m in range(4, 8):
            copy_x(m)
        square_head(0, 0)
        for m in range(4):
            x_emb_transposed(m, 1)
        square_head(0, 1)
        quantise_x(4, 4)
        transpose_and_copy_z(0)
        for u in range(XX_FIRST):
            square_x_emb(u // 2, u % 2)
        quantise_x_emb(0)
        for m in range(4, 8):
            x_emb_transposed(m, 0)
        square_head(0, 2)
        square_head(0, 3)
        norms_z(0)
        transpose_and_copy_z(1)
        for m in range(4, 8):
            x_emb_transposed(m, 1)
        load_z(7)
        square_z(2)
        transpose_z(2)
        for u in range(XX_FIRST, XX_PRO):
            square_x_emb(u // 2, u % 2)
        quantise_z(0)
        copy_z(1, 0)
        copy_z(1, 1)
        quantise_x_emb(1)
        if CL > 3:
            transpose_and_copy_z(3)
        square_z(3)
        norms_z(1)

        transpose_z(CL)
        multiply(0, 0)
        take_head(0, 0, 0 not in H0_ON_V)
        for s in range(15):
            finish = list(FINISH.get(s, []))
            early = s + CL + 1 < 15
            multiply(s, 1)
            if s > 12:
                for k in finish:
                    turn(k)
            multiply(s, 2)
            multiply(s, 3)
            if s < 14:
                multiply(s + 1, 0)
            else:
                multiply_half(15, 0, 0)
            if s + CL + 1 < 16:
                transpose_z(s + CL + 1)
            odd = s % 2
            for k in OWN.get(s, []):
                first_term(k, nc.gpsimd)
            take_head(s, 1, False)
            if s + CL < 16:
                i, heads = half_row(s + CL)
                copy_z(i, heads[0], "scalar" if s in ZC_A else "vector")
                copy_z(i, heads[1], "scalar" if s in ZC_B else "vector")
            if not early and s < 13:
                for k in finish:
                    turn(k)
            if s > 12:
                add_second_term(finish.pop(0))
            if s == 14:
                turn(13)
                turn(14)
            def next_product():
                if s < 14:
                    take_head(s + 1, 0, s + 1 not in H0_ON_V)
                else:
                    take_head(15, 0, False, 0)
            take_head(s, 2, False)
            next_product()
            take_head(s, 3, False)
            if early:
                for k in finish:
                    turn(k, "mx")
            if not odd and s + 3 < 16 and early:
                quantise_z((s + 3) // 2)
            for k in finish:
                add_second_term(k)
            if not odd and not early and s + 3 < 16:
                quantise_z((s + 3) // 2)
            if s in (RX_AT + 1, RX_AT + 2):
                spread_rx(s - RX_AT - 1)
            if s + LA < 16:
                square_z(s + LA)
                if (s + LA) % 2 == 1:
                    norms_z((s + LA) // 2)
            if XX_PRO + s < 16:
                square_x_emb((XX_PRO + s) // 2, (XX_PRO + s) % 2)
            if s in (RX_AT + 1, RX_AT + 2):
                keep_rx_row(s - RX_AT - 1)
            if s == RX_AT - 1:
                nc.gpsimd.tensor_copy(out=beta_f[:], in_=beta_bf[:])
                x_norms()
            for k, last in LOGS.get(s, []):
                logarithm(k, last)
            for k, last in POWERS.get(s, []):
                power(k, last)
                for n in with_blocks:
                    if k <= n <= last:
                        store(n)
        for h in range(1, 4):
            multiply_half(15, h, 0)
        multiply_half(15, 0, 1)
        first_term(14, nc.gpsimd)
        take_head(15, 1, False, 0)
        add_second_term(13)
        take_head(15, 2, False, 0)
        take_head(15, 0, False, 1)
        multiply_half(15, 1, 1)
        multiply_half(15, 2, 1)
        take_head(15, 3, False, 0)
        multiply_half(15, 3, 1)
        add_second_term(14)
        turn(15, "tr", 0, 2)
        take_head(15, 1, False, 1)
        first_term(15, nc.vector, 0, 2)
        take_head(15, 2, False, 1)
        add_second_term(15, 0, 2)
        take_head(15, 3, False, 1)
        logarithm(12, 13)
        logarithm(14)
        logarithm(15, 15, 0, 2)
        mirror(2, "vector")
        first_term(15, nc.vector, 2, 4)
        turn(15, "tr", 2, 4)
        mirror(4, "vector")
        add_second_term(15, 2, 4)
        logarithm(15, 15, 2, 4)
        for k in with_mirror:
            if 4 < k < 12:
                mirror(k, "vector")
        for k in (12, 13, 14):
            power(k)
            store(k)
        for part in range(2):
            power(15, 15, 2 * part, 2 * part + 2)
            store(15, 2 * part, 2 * part + 2)
        for k in (12, 13, 14):
            mirror(k, "vector")
        mirror(15, "vector", 0, 2)
        mirror(15, "vector", 2, 4)
